import numpy as np
import ml_dtypes


def mxq(x, axis, fmt="e4m3"):
    dtype, down = {"e4m3": (ml_dtypes.float8_e4m3fn, 7), "e5m2": (ml_dtypes.float8_e5m2, 14)}[fmt]
    v = np.moveaxis(np.asarray(x, np.float32).astype(ml_dtypes.bfloat16).astype(np.float64), axis, -1)
    blocks = v.reshape(v.shape[:-1] + (-1, 32))
    amax = np.abs(blocks).max(-1, keepdims=True)
    byte = np.maximum(np.where(amax > 0, np.frexp(amax)[1] - 1 + 127, 0) - down, 1)
    scale = np.exp2(byte - 127.0)
    codes = (blocks / scale).astype(np.float32).astype(dtype).astype(np.float64)
    return np.moveaxis((codes * scale).reshape(v.shape), -1, axis)


WIDE = False


def mx_kscale(k):
    if not WIDE:
        return np.ones(k)
    levels = np.array([10, -10, 5, -5, 0])
    a = np.random.permutation(np.resize(levels, k // 512 * 4)).reshape(k // 512, 4)
    idx = np.arange(k)
    return np.exp2(a[idx // 512, idx % 128 // 32])


BF16 = ml_dtypes.bfloat16


def bf(x):
    return np.asarray(x, np.float32).astype(BF16)


def f64(x):
    return np.asarray(x).astype(np.float64)


B, L, S, D, DA, H, MLP = 2, 3, 256, 1024, 1024, 16, 4096
EPS = 1e-5


def layer_norm(u, g, b):
    mu = u.mean(-1, keepdims=True)
    var = ((u - mu) ** 2).mean(-1, keepdims=True)
    return (u - mu) / np.sqrt(var + EPS) * g + b


def setup_inputs():
    s = mx_kscale(DA)
    r = np.random.standard_normal
    return {"h_attn": bf(r((B, S, DA)) * 2.0 * s), "x": bf(r((B, S, D))),
            "attn_out_W": bf(r((DA, D)) * 0.5 / np.sqrt(DA) / s[:, None]), "attn_out_b": bf(r(D) * 0.2),
            "attn_norm_g": bf(1.0 + 0.1 * r(D)), "attn_norm_b": bf(r(D) * 0.1)}


def reference(h_attn, x, attn_out_W, attn_out_b, attn_norm_g, attn_norm_b):
    o = (mxq(f64(h_attn), 2, "e4m3") @ mxq(f64(attn_out_W), 0, "e4m3")) + f64(attn_out_b)
    return f64(x) + layer_norm(o, f64(attn_norm_g), f64(attn_norm_b))

@@ -1,0 +1,257 @@
+from contextlib import ExitStack
+
+import concourse.mybir as mybir
+from concourse.masks import make_identity
+
+F32 = mybir.dt.float32
+BF16 = mybir.dt.bfloat16
+I32 = mybir.dt.int32
+U32 = mybir.dt.uint32
+U8 = mybir.dt.uint8
+FP8X4 = mybir.dt.float8_e4m3fn_x4
+ALU = mybir.AluOpType
+ACT = mybir.ActivationFunctionType
+
+P = 128
+PACK = 4
+PAIR = 2
+K_PASS = P * PACK
+TOKENS = 512
+K = 1024
+FEATURES = 1024
+EPS = 1e-5
+TOKEN_TILES = TOKENS // P
+PASSES = K // K_PASS
+BANK = 512
+HALVES = FEATURES // BANK
+UNITS = PASSES * HALVES
+RUN = 4
+VECTOR_COLS = 344
+VECTORS = 3
+FLOPS = 2 * TOKENS * K * FEATURES
+
+
+def tile_dcadecoderblock_pb_kernel(
+    tc, h_attn, x, attn_out_W, attn_out_b, attn_norm_g, attn_norm_b, out
+):
+    nc = tc.nc
+    h_rows = h_attn.flatten_outer_dims()
+    x_rows = x.flatten_outer_dims()
+    out_rows = out.flatten_outer_dims()
+
+    with ExitStack() as ctx:
+        keep = ctx.enter_context(tc.tile_pool(name="keep", bufs=1))
+        psum = ctx.enter_context(tc.psum_pool(name="psum", bufs=8))
+        ctx.enter_context(tc.manual_schedule())
+
+        h_raw = keep.tile([P, TOKEN_TILES * K], BF16)
+        h_grp = keep.tile([P, TOKEN_TILES * K], BF16, align_bytes=64)
+        h_codes = keep.tile([P, TOKEN_TILES * PASSES * P], U32, align_bytes=64)
+        h_scales = keep.tile([P, TOKEN_TILES * PASSES * P], U8, align_bytes=64)
+        w_raw = keep.tile([P, PASSES, PACK, FEATURES], BF16)
+        w_grp = keep.tile([P, UNITS, BANK, PACK], BF16, align_bytes=64)
+        w_codes = keep.tile([P, UNITS, BANK], U32, align_bytes=64)
+        w_scales = keep.tile([P, UNITS, BANK], U8, align_bytes=64)
+        x_raw = keep.tile([P, TOKEN_TILES, FEATURES], BF16)
+        x_shift = keep.tile([P, TOKEN_TILES, FEATURES], F32)
+        proj = keep.tile([P, TOKEN_TILES, FEATURES], F32)
+        scaled = keep.tile([P, TOKEN_TILES, FEATURES], F32)
+        result = keep.tile([P, TOKEN_TILES, FEATURES], F32)
+        squares = keep.tile([P, TOKEN_TILES, FEATURES], BF16)
+        vec_rows = keep.tile([P, VECTORS * FEATURES], BF16)
+        vec_all = keep.tile([P, VECTORS, FEATURES], BF16)
+        ones = keep.tile([P, P], BF16)
+        ident = keep.tile([P, P], F32)
+        eps = keep.tile([P, 1], F32)
+        warm = keep.tile([P, 1], F32)
+        half_sum = keep.tile([P, TOKEN_TILES * HALVES], F32)
+        neg_mean = keep.tile([P, TOKEN_TILES], F32)
+        sq_sum = keep.tile([P, TOKEN_TILES], F32)
+        std = keep.tile([P, TOKEN_TILES], F32)
+        rstd = keep.tile([P, TOKEN_TILES], F32)
+        bias_all = vec_all[:, 0, :]
+        gain_all = vec_all[:, 1, :]
+        shift_all = vec_all[:, 2, :]
+
+        for v, vec in enumerate((attn_out_b, attn_norm_g, attn_norm_b)):
+            part = slice(v * FEATURES, (v + 1) * FEATURES)
+            nc.vector.memset(vec_rows[:, part].bitcast(I32), 0)
+            nc.scalar.dma_start(out=vec_rows[0:1, part], in_=vec.rearrange("(o c) -> o c", o=1))
+        nc.vector.memset(ones[:], 1.0)
+        nc.vector.memset(eps[:], EPS)
+        make_identity(nc, ident[:])
+        nc.scalar.activation(out=warm[:], in_=eps[:], func=ACT.Sqrt)
+
+        for i in range(TOKEN_TILES):
+            nc.sync.dma_start(out=h_raw[:, i * K : (i + 1) * K], in_=h_rows[i * P : (i + 1) * P, :])
+        for g in range(PASSES):
+            nc.sync.dma_start(
+                out=w_raw[:, g, :, :],
+                in_=attn_out_W[g * K_PASS : (g + 1) * K_PASS, :].rearrange(
+                    "(p t) c -> p t c", t=PACK
+                ),
+            )
+        for i in range(TOKEN_TILES):
+            nc.sync.dma_start(out=x_raw[:, i, :], in_=x_rows[i * P : (i + 1) * P, :])
+
+        h_words = h_raw[:].bitcast(F32).rearrange(
+            "r (i g p u) -> r i g u p", i=TOKEN_TILES, g=PASSES, u=PAIR
+        )
+        h_grp_words = h_grp[:].bitcast(F32).rearrange(
+            "p (i g r u) -> p i g r u", i=TOKEN_TILES, g=PASSES, u=PAIR
+        )
+        for i in range(TOKEN_TILES):
+            flipped = psum.tile([P, BANK], F32, tag="bank", name="flipped")
+            for g in range(PASSES):
+                for u in range(PAIR):
+                    piece = (g * PAIR + u) * P
+                    nc.tensor.transpose(
+                        flipped[:, piece : piece + P], h_words[:, i, g, u, :], ident[:]
+                    )
+            nc.scalar.copy(
+                out=h_grp_words[:, i],
+                in_=flipped[:].rearrange("p (g u r) -> p g r u", g=PASSES, u=PAIR),
+            )
+
+        for v in range(VECTORS):
+            spread = psum.tile([P, FEATURES], BF16, tag="bank", name="spread")
+            for c in range(HALVES):
+                nc.tensor.matmul(
+                    out=spread[:, c * BANK : (c + 1) * BANK],
+                    lhsT=ones[:],
+                    rhs=vec_rows[:, v * FEATURES + c * BANK : v * FEATURES + (c + 1) * BANK],
+                    start=True,
+                    stop=True,
+                )
+            nc.scalar.copy(out=vec_all[:, v, :], in_=spread[:])
+
+        for i in range(TOKEN_TILES):
+            words = slice(i * PASSES * P, (i + 1) * PASSES * P)
+            nc.vector.quantize_mx(
+                out=h_codes[:, words].bitcast(FP8X4),
+                scales=h_scales[:, words],
+                in_=h_grp[:, i * K : (i + 1) * K],
+            )
+
+        for i in range(TOKEN_TILES):
+            nc.gpsimd.tensor_tensor(
+                out=x_shift[:, i, :], in0=x_raw[:, i, :], in1=shift_all, op=ALU.add
+            )
+
+        def regroup(unit):
+            g, c = divmod(unit, HALVES)
+            src = w_raw[:, g, :, c * BANK : (c + 1) * BANK].rearrange(
+                "p t (c i) -> p c t i", i=RUN
+            )
+            dst = w_grp[:, unit, :, :].rearrange("p (c i) t -> p c t i", i=RUN)
+            cut = VECTOR_COLS // RUN
+            nc.vector.tensor_copy(out=dst[:, :cut], in_=src[:, :cut])
+            nc.scalar.copy(out=dst[:, cut:], in_=src[:, cut:])
+
+        def quantise(unit):
+            nc.vector.quantize_mx(
+                out=w_codes[:, unit, :].bitcast(FP8X4),
+                scales=w_scales[:, unit, :],
+                in_=w_grp[:, unit, :, :].rearrange("p c t -> p (c t)"),
+            )
+
+        acc = [
+            [psum.tile([P, BANK], F32, tag="bank", name="acc") for c in range(HALVES)]
+            for i in range(TOKEN_TILES)
+        ]
+
+        def multiply(unit):
+            g, c = divmod(unit, HALVES)
+            for i in range(TOKEN_TILES):
+                words = slice((i * PASSES + g) * P, (i * PASSES + g + 1) * P)
+                nc.tensor.matmul_mx(
+                    out=acc[i][c][:],
+                    lhsT=h_codes[:, words].bitcast(FP8X4),
+                    lhsT_scale=h_scales[:, words],
+                    rhs=w_codes[:, unit, :].bitcast(FP8X4),
+                    rhs_scale=w_scales[:, unit, :],
+                    start=(g == 0),
+                    stop=(g == PASSES - 1),
+                )
+
+        def add_bias(i, c):
+            cols = slice(c * BANK, (c + 1) * BANK)
+            nc.vector.scalar_tensor_tensor(
+                out=proj[:, i, cols],
+                in0=acc[i][c][:],
+                scalar=1.0,
+                in1=bias_all[:, cols],
+                op0=ALU.mult,
+                op1=ALU.add,
+                accum_out=half_sum[:, i * HALVES + c : i * HALVES + c + 1],
+            )
+
+        regroup(0)
+        for unit in range(UNITS):
+            if unit + 1 < UNITS:
+                regroup(unit + 1)
+            quantise(unit)
+            multiply(unit)
+
+        def mean(i):
+            nc.vector.tensor_scalar(
+                out=neg_mean[:, i : i + 1],
+                in0=half_sum[:, i * HALVES : i * HALVES + 1],
+                scalar1=half_sum[:, i * HALVES + 1 : i * HALVES + 2],
+                scalar2=-1.0 / FEATURES,
+                op0=ALU.add,
+                op1=ALU.mult,
+            )
+
+        def deviation(i):
+            nc.scalar.activation(
+                out=squares[:, i, :],
+                in_=proj[:, i, :],
+                func=ACT.Square,
+                bias=neg_mean[:, i : i + 1],
+                scale=1.0,
+                accum_out=sq_sum[:, i : i + 1],
+            )
+            nc.scalar.activation(
+                out=std[:, i : i + 1],
+                in_=sq_sum[:, i : i + 1],
+                func=ACT.Sqrt,
+                bias=eps[:],
+                scale=1.0 / FEATURES,
+            )
+
+        def centre_and_gain(i):
+            nc.vector.scalar_tensor_tensor(
+                out=scaled[:, i, :],
+                in0=proj[:, i, :],
+                scalar=neg_mean[:, i : i + 1],
+                in1=gain_all,
+                op0=ALU.add,
+                op1=ALU.mult,
+            )
+
+        def finish(i):
+            nc.vector.scalar_tensor_tensor(
+                out=result[:, i, :],
+                in0=scaled[:, i, :],
+                scalar=rstd[:, i : i + 1],
+                in1=x_shift[:, i, :],
+                op0=ALU.mult,
+                op1=ALU.add,
+            )
+            nc.sync.dma_start(out=out_rows[i * P : (i + 1) * P, :], in_=result[:, i, :])
+
+        for step in range(TOKEN_TILES + 2):
+            first, second, third = step, step - 1, step - 2
+            if 0 <= second < TOKEN_TILES:
+                mean(second)
+                deviation(second)
+            if 0 <= third < TOKEN_TILES:
+                nc.vector.reciprocal(out=rstd[:, third : third + 1], in_=std[:, third : third + 1])
+            if first < TOKEN_TILES:
+                for c in range(HALVES):
+                    add_bias(first, c)
+            if 0 <= second < TOKEN_TILES:
+                centre_and_gain(second)
+            if 0 <= third < TOKEN_TILES:
+                finish(third)

@@ -144,9 +144,12 @@ def tile_dcadecoderblock_pb_kernel(
                 "p t (c i) -> p c t i", i=RUN
             )
             dst = w_grp[:, unit, :, :].rearrange("p (c i) t -> p c t i", i=RUN)
-            cut = VECTOR_COLS // RUN
-            nc.vector.tensor_copy(out=dst[:, :cut], in_=src[:, :cut])
-            nc.scalar.copy(out=dst[:, cut:], in_=src[:, cut:])
+            if g == 0:
+                nc.vector.tensor_copy(out=dst, in_=src)
+            else:
+                cut = VECTOR_COLS // RUN
+                nc.vector.tensor_copy(out=dst[:, :cut], in_=src[:, :cut])
+                nc.scalar.copy(out=dst[:, cut:], in_=src[:, cut:])
 
         def quantise(unit):
             nc.vector.quantize_mx(
@@ -160,19 +163,18 @@ def tile_dcadecoderblock_pb_kernel(
             for i in range(TOKEN_TILES)
         ]
 
-        def multiply(unit):
+        def multiply(i, unit):
             g, c = divmod(unit, HALVES)
-            for i in range(TOKEN_TILES):
-                words = slice((i * PASSES + g) * P, (i * PASSES + g + 1) * P)
-                nc.tensor.matmul_mx(
-                    out=acc[i][c][:],
-                    lhsT=h_codes[:, words].bitcast(FP8X4),
-                    lhsT_scale=h_scales[:, words],
-                    rhs=w_codes[:, unit, :].bitcast(FP8X4),
-                    rhs_scale=w_scales[:, unit, :],
-                    start=(g == 0),
-                    stop=(g == PASSES - 1),
-                )
+            words = slice((i * PASSES + g) * P, (i * PASSES + g + 1) * P)
+            nc.tensor.matmul_mx(
+                out=acc[i][c][:],
+                lhsT=h_codes[:, words].bitcast(FP8X4),
+                lhsT_scale=h_scales[:, words],
+                rhs=w_codes[:, unit, :].bitcast(FP8X4),
+                rhs_scale=w_scales[:, unit, :],
+                start=(g == 0),
+                stop=(g == PASSES - 1),
+            )
 
         def add_bias(i, c):
             cols = slice(c * BANK, (c + 1) * BANK)
@@ -186,12 +188,18 @@ def tile_dcadecoderblock_pb_kernel(
                 accum_out=half_sum[:, i * HALVES + c : i * HALVES + c + 1],
             )
 
+        last_pass = range(UNITS - HALVES, UNITS)
         regroup(0)
         for unit in range(UNITS):
             if unit + 1 < UNITS:
                 regroup(unit + 1)
             quantise(unit)
-            multiply(unit)
+            if unit not in last_pass:
+                for i in range(TOKEN_TILES):
+                    multiply(i, unit)
+        for i in range(TOKEN_TILES):
+            for unit in last_pass:
+                multiply(i, unit)
 
         def mean(i):
             nc.vector.tensor_scalar(
@@ -231,15 +239,17 @@ def tile_dcadecoderblock_pb_kernel(
             )
 
         def finish(i):
-            nc.vector.scalar_tensor_tensor(
-                out=result[:, i, :],
-                in0=scaled[:, i, :],
-                scalar=rstd[:, i : i + 1],
-                in1=x_shift[:, i, :],
-                op0=ALU.mult,
-                op1=ALU.add,
-            )
-            nc.sync.dma_start(out=out_rows[i * P : (i + 1) * P, :], in_=result[:, i, :])
+            for c in range(HALVES):
+                cols = slice(c * BANK, (c + 1) * BANK)
+                nc.vector.scalar_tensor_tensor(
+                    out=result[:, i, cols],
+                    in0=scaled[:, i, cols],
+                    scalar=rstd[:, i : i + 1],
+                    in1=x_shift[:, i, cols],
+                    op0=ALU.mult,
+                    op1=ALU.add,
+                )
+                nc.sync.dma_start(out=out_rows[i * P : (i + 1) * P, cols], in_=result[:, i, cols])
 
         for step in range(TOKEN_TILES + 2):
             first, second, third = step, step - 1, step - 2

@@ -133,11 +133,6 @@ def tile_dcadecoderblock_pb_kernel(
                 in_=h_grp[:, i * K : (i + 1) * K],
             )
 
-        for i in range(TOKEN_TILES):
-            nc.gpsimd.tensor_tensor(
-                out=x_shift[:, i, :], in0=x_raw[:, i, :], in1=shift_all, op=ALU.add
-            )
-
         def regroup(unit):
             g, c = divmod(unit, HALVES)
             src = w_raw[:, g, :, c * BANK : (c + 1) * BANK].rearrange(
@@ -228,6 +223,11 @@ def tile_dcadecoderblock_pb_kernel(
                 scale=1.0 / FEATURES,
             )
 
+        def add_shift(i):
+            nc.vector.tensor_tensor(
+                out=x_shift[:, i, :], in0=x_raw[:, i, :], in1=shift_all, op=ALU.add
+            )
+
         def centre_and_gain(i):
             nc.vector.scalar_tensor_tensor(
                 out=scaled[:, i, :],
@@ -262,6 +262,7 @@ def tile_dcadecoderblock_pb_kernel(
                 for c in range(HALVES):
                     add_bias(first, c)
             if 0 <= second < TOKEN_TILES:
+                add_shift(second)
                 centre_and_gain(second)
             if 0 <= third < TOKEN_TILES:
                 finish(third)

@@ -26,8 +26,8 @@ BANK = 512
 HALVES = FEATURES // BANK
 UNITS = PASSES * HALVES
 RUN = 4
-VECTOR_COLS = 344
 VECTORS = 3
+QUADRANT = 32
 FLOPS = 2 * TOKENS * K * FEATURES
 
 
@@ -38,6 +38,8 @@ def tile_dcadecoderblock_pb_kernel(
     h_rows = h_attn.flatten_outer_dims()
     x_rows = x.flatten_outer_dims()
     out_rows = out.flatten_outer_dims()
+    first_pass = range(HALVES)
+    last_pass = range(UNITS - HALVES, UNITS)
 
     with ExitStack() as ctx:
         keep = ctx.enter_context(tc.tile_pool(name="keep", bufs=1))
@@ -48,7 +50,7 @@ def tile_dcadecoderblock_pb_kernel(
         h_grp = keep.tile([P, TOKEN_TILES * K], BF16, align_bytes=64)
         h_codes = keep.tile([P, TOKEN_TILES * PASSES * P], U32, align_bytes=64)
         h_scales = keep.tile([P, TOKEN_TILES * PASSES * P], U8, align_bytes=64)
-        w_raw = keep.tile([P, PASSES, PACK, FEATURES], BF16)
+        w_raw = keep.tile([P, UNITS, PACK, BANK], BF16)
         w_grp = keep.tile([P, UNITS, BANK, PACK], BF16, align_bytes=64)
         w_codes = keep.tile([P, UNITS, BANK], U32, align_bytes=64)
         w_scales = keep.tile([P, UNITS, BANK], U8, align_bytes=64)
@@ -58,41 +60,101 @@ def tile_dcadecoderblock_pb_kernel(
         scaled = keep.tile([P, TOKEN_TILES, FEATURES], F32)
         result = keep.tile([P, TOKEN_TILES, FEATURES], F32)
         squares = keep.tile([P, TOKEN_TILES, FEATURES], BF16)
-        vec_rows = keep.tile([P, VECTORS * FEATURES], BF16)
+        vec_rows = keep.tile([P, FEATURES], BF16)
         vec_all = keep.tile([P, VECTORS, FEATURES], BF16)
-        ones = keep.tile([P, P], BF16)
+        pick = keep.tile([P, VECTORS * P], BF16)
         ident = keep.tile([P, P], F32)
         eps = keep.tile([P, 1], F32)
         warm = keep.tile([P, 1], F32)
         half_sum = keep.tile([P, TOKEN_TILES * HALVES], F32)
+        half_mean = keep.tile([P, TOKEN_TILES * HALVES], F32)
         neg_mean = keep.tile([P, TOKEN_TILES], F32)
         sq_sum = keep.tile([P, TOKEN_TILES], F32)
-        std = keep.tile([P, TOKEN_TILES], F32)
         rstd = keep.tile([P, TOKEN_TILES], F32)
-        bias_all = vec_all[:, 0, :]
-        gain_all = vec_all[:, 1, :]
-        shift_all = vec_all[:, 2, :]
+        shift_all = vec_all[:, 0, :]
+        bias_all = vec_all[:, 1, :]
+        gain_all = vec_all[:, 2, :]
 
-        for v, vec in enumerate((attn_out_b, attn_norm_g, attn_norm_b)):
-            part = slice(v * FEATURES, (v + 1) * FEATURES)
-            nc.vector.memset(vec_rows[:, part].bitcast(I32), 0)
-            nc.scalar.dma_start(out=vec_rows[0:1, part], in_=vec.rearrange("(o c) -> o c", o=1))
-        nc.vector.memset(ones[:], 1.0)
-        nc.vector.memset(eps[:], EPS)
-        make_identity(nc, ident[:])
-        nc.scalar.activation(out=warm[:], in_=eps[:], func=ACT.Sqrt)
+        def load_weight(unit):
+            g, c = divmod(unit, HALVES)
+            nc.sync.dma_start(
+                out=w_raw[:, unit, :, :],
+                in_=attn_out_W[
+                    g * K_PASS : (g + 1) * K_PASS, c * BANK : (c + 1) * BANK
+                ].rearrange("(p t) c -> p t c", t=PACK),
+            )
 
+        def load_x(i):
+            nc.sync.dma_start(out=x_raw[:, i, :], in_=x_rows[i * P : (i + 1) * P, :])
+
+        load_weight(first_pass[0])
+        nc.vector.memset(vec_rows[:].bitcast(I32), 0)
+        for v, vec in enumerate((attn_norm_b, attn_out_b, attn_norm_g)):
+            row = v * QUADRANT
+            nc.sync.dma_start(
+                out=vec_rows[row : row + 1, :], in_=vec.rearrange("(o c) -> o c", o=1)
+            )
+        x_share = TOKEN_TILES // HALVES
+        load_weight(first_pass[1])
+        load_weight(last_pass[0])
+        for i in range(x_share):
+            load_x(i)
         for i in range(TOKEN_TILES):
             nc.sync.dma_start(out=h_raw[:, i * K : (i + 1) * K], in_=h_rows[i * P : (i + 1) * P, :])
-        for g in range(PASSES):
-            nc.sync.dma_start(
-                out=w_raw[:, g, :, :],
-                in_=attn_out_W[g * K_PASS : (g + 1) * K_PASS, :].rearrange(
-                    "(p t) c -> p t c", t=PACK
-                ),
+        load_weight(last_pass[1])
+        for i in range(x_share, TOKEN_TILES):
+            load_x(i)
+
+        nc.vector.memset(pick[:].bitcast(I32), 0)
+        for v in range(VECTORS):
+            row = v * QUADRANT
+            nc.vector.memset(pick[row : row + 1, v * P : (v + 1) * P], 1.0)
+        nc.vector.memset(eps[:], EPS)
+        make_identity(nc, ident[:])
+        nc.scalar.activation(out=warm[:], in_=eps[:], func=ACT.Abs_reciprocal_sqrt)
+
+        for v in range(VECTORS):
+            spread = psum.tile([P, FEATURES], BF16, tag="bank", name="spread")
+            for c in range(HALVES):
+                nc.tensor.matmul(
+                    out=spread[:, c * BANK : (c + 1) * BANK],
+                    lhsT=pick[:, v * P : (v + 1) * P],
+                    rhs=vec_rows[:, c * BANK : (c + 1) * BANK],
+                    start=True,
+                    stop=True,
+                )
+            nc.scalar.copy(out=vec_all[:, v, :], in_=spread[:])
+
+        def regroup(copy, unit):
+            copy(
+                out=w_grp[:, unit, :, :].rearrange("p (c i) t -> p c t i", i=RUN),
+                in_=w_raw[:, unit, :, :].rearrange("p t (c i) -> p c t i", i=RUN),
             )
-        for i in range(TOKEN_TILES):
-            nc.sync.dma_start(out=x_raw[:, i, :], in_=x_rows[i * P : (i + 1) * P, :])
+
+        def quantise(unit):
+            nc.vector.quantize_mx(
+                out=w_codes[:, unit, :].bitcast(FP8X4),
+                scales=w_scales[:, unit, :],
+                in_=w_grp[:, unit, :, :].rearrange("p c t -> p (c t)"),
+            )
+
+        def add_shift(i):
+            nc.vector.tensor_tensor(
+                out=x_shift[:, i, :], in0=x_raw[:, i, :], in1=shift_all, op=ALU.add
+            )
+
+        for unit in first_pass:
+            regroup(nc.vector.tensor_copy, unit)
+        for unit in first_pass:
+            quantise(unit)
+
+        def scalar_unit(n):
+            regroup(nc.scalar.copy, last_pass[n])
+            for i in range(n * x_share, (n + 1) * x_share):
+                add_shift(i)
+            quantise(last_pass[n])
+
+        scalar_unit(0)
 
         h_words = h_raw[:].bitcast(F32).rearrange(
             "r (i g p u) -> r i g u p", i=TOKEN_TILES, g=PASSES, u=PAIR
@@ -112,45 +174,12 @@ def tile_dcadecoderblock_pb_kernel(
                 out=h_grp_words[:, i],
                 in_=flipped[:].rearrange("p (g u r) -> p g r u", g=PASSES, u=PAIR),
             )
-
-        for v in range(VECTORS):
-            spread = psum.tile([P, FEATURES], BF16, tag="bank", name="spread")
-            for c in range(HALVES):
-                nc.tensor.matmul(
-                    out=spread[:, c * BANK : (c + 1) * BANK],
-                    lhsT=ones[:],
-                    rhs=vec_rows[:, v * FEATURES + c * BANK : v * FEATURES + (c + 1) * BANK],
-                    start=True,
-                    stop=True,
-                )
-            nc.scalar.copy(out=vec_all[:, v, :], in_=spread[:])
-
         for i in range(TOKEN_TILES):
             words = slice(i * PASSES * P, (i + 1) * PASSES * P)
             nc.vector.quantize_mx(
                 out=h_codes[:, words].bitcast(FP8X4),
                 scales=h_scales[:, words],
                 in_=h_grp[:, i * K : (i + 1) * K],
-            )
-
-        def regroup(unit):
-            g, c = divmod(unit, HALVES)
-            src = w_raw[:, g, :, c * BANK : (c + 1) * BANK].rearrange(
-                "p t (c i) -> p c t i", i=RUN
-            )
-            dst = w_grp[:, unit, :, :].rearrange("p (c i) t -> p c t i", i=RUN)
-            if g == 0:
-                nc.vector.tensor_copy(out=dst, in_=src)
-            else:
-                cut = VECTOR_COLS // RUN
-                nc.vector.tensor_copy(out=dst[:, :cut], in_=src[:, :cut])
-                nc.scalar.copy(out=dst[:, cut:], in_=src[:, cut:])
-
-        def quantise(unit):
-            nc.vector.quantize_mx(
-                out=w_codes[:, unit, :].bitcast(FP8X4),
-                scales=w_scales[:, unit, :],
-                in_=w_grp[:, unit, :, :].rearrange("p c t -> p (c t)"),
             )
 
         acc = [
@@ -171,42 +200,37 @@ def tile_dcadecoderblock_pb_kernel(
                 stop=(g == PASSES - 1),
             )
 
-        def add_bias(i, c):
-            cols = slice(c * BANK, (c + 1) * BANK)
-            nc.vector.scalar_tensor_tensor(
-                out=proj[:, i, cols],
-                in0=acc[i][c][:],
-                scalar=1.0,
-                in1=bias_all[:, cols],
-                op0=ALU.mult,
-                op1=ALU.add,
-                accum_out=half_sum[:, i * HALVES + c : i * HALVES + c + 1],
-            )
+        for unit in first_pass:
+            for i in range(TOKEN_TILES):
+                multiply(i, unit)
 
-        last_pass = range(UNITS - HALVES, UNITS)
-        regroup(0)
-        for unit in range(UNITS):
-            if unit + 1 < UNITS:
-                regroup(unit + 1)
-            quantise(unit)
-            if unit not in last_pass:
-                for i in range(TOKEN_TILES):
-                    multiply(i, unit)
+        scalar_unit(1)
         for i in range(TOKEN_TILES):
             for unit in last_pass:
                 multiply(i, unit)
 
-        def mean(i):
-            nc.vector.tensor_scalar(
-                out=neg_mean[:, i : i + 1],
-                in0=half_sum[:, i * HALVES : i * HALVES + 1],
-                scalar1=half_sum[:, i * HALVES + 1 : i * HALVES + 2],
-                scalar2=-1.0 / FEATURES,
-                op0=ALU.add,
-                op1=ALU.mult,
-            )
+        def add_bias(i):
+            for c in range(HALVES):
+                cols = slice(c * BANK, (c + 1) * BANK)
+                nc.vector.scalar_tensor_tensor(
+                    out=proj[:, i, cols],
+                    in0=acc[i][c][:],
+                    scalar=1.0,
+                    in1=bias_all[:, cols],
+                    op0=ALU.mult,
+                    op1=ALU.add,
+                    accum_out=half_sum[:, i * HALVES + c : i * HALVES + c + 1],
+                )
 
-        def deviation(i):
+        def statistics(i):
+            halves = slice(i * HALVES, (i + 1) * HALVES)
+            nc.scalar.activation(
+                out=half_mean[:, halves],
+                in_=half_sum[:, halves],
+                func=ACT.Copy,
+                scale=-1.0 / FEATURES,
+                accum_out=neg_mean[:, i : i + 1],
+            )
             nc.scalar.activation(
                 out=squares[:, i, :],
                 in_=proj[:, i, :],
@@ -216,16 +240,11 @@ def tile_dcadecoderblock_pb_kernel(
                 accum_out=sq_sum[:, i : i + 1],
             )
             nc.scalar.activation(
-                out=std[:, i : i + 1],
+                out=rstd[:, i : i + 1],
                 in_=sq_sum[:, i : i + 1],
-                func=ACT.Sqrt,
+                func=ACT.Abs_reciprocal_sqrt,
                 bias=eps[:],
                 scale=1.0 / FEATURES,
-            )
-
-        def add_shift(i):
-            nc.vector.tensor_tensor(
-                out=x_shift[:, i, :], in0=x_raw[:, i, :], in1=shift_all, op=ALU.add
             )
 
         def centre_and_gain(i):
@@ -253,16 +272,10 @@ def tile_dcadecoderblock_pb_kernel(
 
         for step in range(TOKEN_TILES + 2):
             first, second, third = step, step - 1, step - 2
-            if 0 <= second < TOKEN_TILES:
-                mean(second)
-                deviation(second)
-            if 0 <= third < TOKEN_TILES:
-                nc.vector.reciprocal(out=rstd[:, third : third + 1], in_=std[:, third : third + 1])
             if first < TOKEN_TILES:
-                for c in range(HALVES):
-                    add_bias(first, c)
+                add_bias(first)
+                statistics(first)
             if 0 <= second < TOKEN_TILES:
-                add_shift(second)
                 centre_and_gain(second)
             if 0 <= third < TOKEN_TILES:
                 finish(third)

@@ -26,8 +26,9 @@ BANK = 512
 HALVES = FEATURES // BANK
 UNITS = PASSES * HALVES
 RUN = 4
-VECTORS = 3
 QUADRANT = 32
+BLOCKS = FEATURES // P
+BANK_BLOCKS = BANK // P
 FLOPS = 2 * TOKENS * K * FEATURES
 
 
@@ -35,15 +36,43 @@ def tile_dcadecoderblock_pb_kernel(
     tc, h_attn, x, attn_out_W, attn_out_b, attn_norm_g, attn_norm_b, out
 ):
     nc = tc.nc
+    tiles = range(TOKEN_TILES)
+    early, late = 320, 256
+
+    def both(name, i):
+        return [(name, i, 0), (name, i, 1)]
+
+    BANKS = {("spread", 0): 0, ("spread", 2): 1, ("spread", 1): 6}
+    for i in tiles:
+        BANKS["h", i] = 2 + i
+        BANKS["acc", i, 0] = (6, 0, 2, 4)[i]
+        BANKS["acc", i, 1] = (7, 1, 3, 5)[i]
+    LOADS = [("w", 0), ("v",), ("w", 1)] + [("h", i) for i in tiles] + [("w", 2), ("w", 3)] + [("x", i) for i in tiles]
+    HEAD = (
+        [("rg", "V", 0, 0, early), ("rg", "S", 0, early, BANK), ("vp", 0), ("vp", 2), ("rg", "V", 1, 0, early), ("rg", "S", 1, early, BANK)]
+        + [("vo", 0), ("vo", 2), ("q", 0), ("q", 1)] + [("fh", i) for i in tiles] + [("ch", i) for i in tiles]
+        + [step for i in tiles for step in (("qh", i), ("mm", i, 0), ("mm", i, 1))]
+        + [("rg", "S", 2, late, BANK), ("rg", "S", 3, late, BANK), ("rg", "V", 2, 0, late), ("rg", "V", 3, 0, late)]
+        + [("q", 2), ("q", 3), ("go",)] + [("mm", i, u) for i in tiles for u in (2, 3)]
+    )
+    ORDER = (
+        [step for i in tiles for step in both("E", i)]
+        + both("A", 0) + [("mu", 0), ("var", 0), ("vp", 1)]
+        + [step for i in tiles[1:] for step in both("A", i) + [("mu", i), ("var", i)]]
+        + [("C", i) for i in tiles]
+        + [step for i in tiles for step in both("D", i)]
+    )
     h_rows = h_attn.flatten_outer_dims()
     x_rows = x.flatten_outer_dims()
     out_rows = out.flatten_outer_dims()
-    first_pass = range(HALVES)
-    last_pass = range(UNITS - HALVES, UNITS)
 
     with ExitStack() as ctx:
         keep = ctx.enter_context(tc.tile_pool(name="keep", bufs=1))
-        psum = ctx.enter_context(tc.psum_pool(name="psum", bufs=8))
+        psum = ctx.enter_context(tc.psum_pool(name="psum", bufs=1))
+
+        def bank_tile(k, shape, dtype):
+            return psum.tile(shape, dtype, tag="bank%d" % k, name="bank%d" % k)
+
         ctx.enter_context(tc.manual_schedule())
 
         h_raw = keep.tile([P, TOKEN_TILES * K], BF16)
@@ -55,14 +84,15 @@ def tile_dcadecoderblock_pb_kernel(
         w_codes = keep.tile([P, UNITS, BANK], U32, align_bytes=64)
         w_scales = keep.tile([P, UNITS, BANK], U8, align_bytes=64)
         x_raw = keep.tile([P, TOKEN_TILES, FEATURES], BF16)
-        x_shift = keep.tile([P, TOKEN_TILES, FEATURES], F32)
         proj = keep.tile([P, TOKEN_TILES, FEATURES], F32)
         scaled = keep.tile([P, TOKEN_TILES, FEATURES], F32)
+        x_shift = keep.tile([P, TOKEN_TILES, FEATURES], F32)
+        shift_all = keep.tile([P, FEATURES], BF16)
         result = keep.tile([P, TOKEN_TILES, FEATURES], F32)
         squares = keep.tile([P, TOKEN_TILES, FEATURES], BF16)
         vec_rows = keep.tile([P, FEATURES], BF16)
-        vec_all = keep.tile([P, VECTORS, FEATURES], BF16)
-        pick = keep.tile([P, VECTORS * P], BF16)
+        bias_all = keep.tile([P, FEATURES], BF16)
+        pick = keep.tile([P, 3 * P], BF16)
         ident = keep.tile([P, P], F32)
         eps = keep.tile([P, 1], F32)
         warm = keep.tile([P, 1], F32)
@@ -71,9 +101,6 @@ def tile_dcadecoderblock_pb_kernel(
         neg_mean = keep.tile([P, TOKEN_TILES], F32)
         sq_sum = keep.tile([P, TOKEN_TILES], F32)
         rstd = keep.tile([P, TOKEN_TILES], F32)
-        shift_all = vec_all[:, 0, :]
-        bias_all = vec_all[:, 1, :]
-        gain_all = vec_all[:, 2, :]
 
         def load_weight(unit):
             g, c = divmod(unit, HALVES)
@@ -84,51 +111,37 @@ def tile_dcadecoderblock_pb_kernel(
                 ].rearrange("(p t) c -> p t c", t=PACK),
             )
 
+        def load_h(i):
+            nc.sync.dma_start(out=h_raw[:, i * K : (i + 1) * K], in_=h_rows[i * P : (i + 1) * P, :])
+
+        def load_vecs():
+            for v, vec in enumerate((attn_out_b, attn_norm_g, attn_norm_b)):
+                row = v * QUADRANT
+                nc.sync.dma_start(
+                    out=vec_rows[row : row + 1, :], in_=vec.rearrange("(o c) -> o c", o=1)
+                )
+
         def load_x(i):
             nc.sync.dma_start(out=x_raw[:, i, :], in_=x_rows[i * P : (i + 1) * P, :])
 
-        load_weight(first_pass[0])
         nc.vector.memset(vec_rows[:].bitcast(I32), 0)
-        for v, vec in enumerate((attn_norm_b, attn_out_b, attn_norm_g)):
-            row = v * QUADRANT
-            nc.sync.dma_start(
-                out=vec_rows[row : row + 1, :], in_=vec.rearrange("(o c) -> o c", o=1)
-            )
-        x_share = TOKEN_TILES // HALVES
-        load_weight(first_pass[1])
-        load_weight(last_pass[0])
-        for i in range(x_share):
-            load_x(i)
-        for i in range(TOKEN_TILES):
-            nc.sync.dma_start(out=h_raw[:, i * K : (i + 1) * K], in_=h_rows[i * P : (i + 1) * P, :])
-        load_weight(last_pass[1])
-        for i in range(x_share, TOKEN_TILES):
-            load_x(i)
+        loaders = dict(w=load_weight, h=load_h, v=lambda: load_vecs(), x=load_x)
+        for op in LOADS:
+            loaders[op[0]](*op[1:])
 
         nc.vector.memset(pick[:].bitcast(I32), 0)
-        for v in range(VECTORS):
-            row = v * QUADRANT
-            nc.vector.memset(pick[row : row + 1, v * P : (v + 1) * P], 1.0)
+        nc.vector.memset(pick[0:1, 0:P], 1.0)
+        nc.vector.memset(pick[QUADRANT : QUADRANT + 1, P : 2 * P], 1.0)
+        nc.vector.memset(pick[2 * QUADRANT : 2 * QUADRANT + 1, 2 * P : 3 * P], 1.0)
         nc.vector.memset(eps[:], EPS)
         make_identity(nc, ident[:])
         nc.scalar.activation(out=warm[:], in_=eps[:], func=ACT.Abs_reciprocal_sqrt)
 
-        for v in range(VECTORS):
-            spread = psum.tile([P, FEATURES], BF16, tag="bank", name="spread")
-            for c in range(HALVES):
-                nc.tensor.matmul(
-                    out=spread[:, c * BANK : (c + 1) * BANK],
-                    lhsT=pick[:, v * P : (v + 1) * P],
-                    rhs=vec_rows[:, c * BANK : (c + 1) * BANK],
-                    start=True,
-                    stop=True,
-                )
-            nc.scalar.copy(out=vec_all[:, v, :], in_=spread[:])
-
-        def regroup(copy, unit):
+        def regroup(eng, unit, lo, hi):
+            copy = nc.vector.tensor_copy if eng == "V" else nc.scalar.copy
             copy(
-                out=w_grp[:, unit, :, :].rearrange("p (c i) t -> p c t i", i=RUN),
-                in_=w_raw[:, unit, :, :].rearrange("p t (c i) -> p c t i", i=RUN),
+                out=w_grp[:, unit, lo:hi, :].rearrange("p (c i) t -> p c t i", i=RUN),
+                in_=w_raw[:, unit, :, lo:hi].rearrange("p t (c i) -> p c t i", i=RUN),
             )
 
         def quantise(unit):
@@ -138,43 +151,47 @@ def tile_dcadecoderblock_pb_kernel(
                 in_=w_grp[:, unit, :, :].rearrange("p c t -> p (c t)"),
             )
 
-        def add_shift(i):
-            nc.vector.tensor_tensor(
-                out=x_shift[:, i, :], in0=x_raw[:, i, :], in1=shift_all, op=ALU.add
-            )
+        def vectors_pe(v):
+            spread = bank_tile(BANKS["spread", v], [P, FEATURES], BF16)
+            for c in range(HALVES):
+                nc.tensor.matmul(
+                    out=spread[:, c * BANK : (c + 1) * BANK],
+                    lhsT=pick[:, v * P : (v + 1) * P],
+                    rhs=vec_rows[:, c * BANK : (c + 1) * BANK],
+                    start=True,
+                    stop=True,
+                )
+            held["spread", v] = spread
 
-        for unit in first_pass:
-            regroup(nc.vector.tensor_copy, unit)
-        for unit in first_pass:
-            quantise(unit)
+        def vectors_out(v):
+            nc.scalar.copy(out=(bias_all if v == 0 else shift_all)[:], in_=held["spread", v][:])
 
-        def scalar_unit(n):
-            regroup(nc.scalar.copy, last_pass[n])
-            for i in range(n * x_share, (n + 1) * x_share):
-                add_shift(i)
-            quantise(last_pass[n])
-
-        scalar_unit(0)
-
+        held = {}
         h_words = h_raw[:].bitcast(F32).rearrange(
             "r (i g p u) -> r i g u p", i=TOKEN_TILES, g=PASSES, u=PAIR
         )
         h_grp_words = h_grp[:].bitcast(F32).rearrange(
             "p (i g r u) -> p i g r u", i=TOKEN_TILES, g=PASSES, u=PAIR
         )
-        for i in range(TOKEN_TILES):
-            flipped = psum.tile([P, BANK], F32, tag="bank", name="flipped")
+
+        def flip_h(i):
+            flipped = bank_tile(BANKS["h", i], [P, BANK], F32)
             for g in range(PASSES):
                 for u in range(PAIR):
                     piece = (g * PAIR + u) * P
                     nc.tensor.transpose(
                         flipped[:, piece : piece + P], h_words[:, i, g, u, :], ident[:]
                     )
-            nc.scalar.copy(
+            held["h", i] = flipped
+
+        def copy_h(i, eng="S"):
+            copy = nc.vector.tensor_copy if eng == "V" else nc.scalar.copy
+            copy(
                 out=h_grp_words[:, i],
-                in_=flipped[:].rearrange("p (g u r) -> p g r u", g=PASSES, u=PAIR),
+                in_=held["h", i][:].rearrange("p (g u r) -> p g r u", g=PASSES, u=PAIR),
             )
-        for i in range(TOKEN_TILES):
+
+        def quantise_h(i):
             words = slice(i * PASSES * P, (i + 1) * PASSES * P)
             nc.vector.quantize_mx(
                 out=h_codes[:, words].bitcast(FP8X4),
@@ -182,16 +199,15 @@ def tile_dcadecoderblock_pb_kernel(
                 in_=h_grp[:, i * K : (i + 1) * K],
             )
 
-        acc = [
-            [psum.tile([P, BANK], F32, tag="bank", name="acc") for c in range(HALVES)]
-            for i in range(TOKEN_TILES)
-        ]
+        acc = {}
 
         def multiply(i, unit):
             g, c = divmod(unit, HALVES)
+            if g == 0:
+                acc[i, c] = bank_tile(BANKS["acc", i, c], [P, BANK], F32)
             words = slice((i * PASSES + g) * P, (i * PASSES + g + 1) * P)
             nc.tensor.matmul_mx(
-                out=acc[i][c][:],
+                out=acc[i, c][:],
                 lhsT=h_codes[:, words].bitcast(FP8X4),
                 lhsT_scale=h_scales[:, words],
                 rhs=w_codes[:, unit, :].bitcast(FP8X4),
@@ -200,29 +216,28 @@ def tile_dcadecoderblock_pb_kernel(
                 stop=(g == PASSES - 1),
             )
 
-        for unit in first_pass:
-            for i in range(TOKEN_TILES):
-                multiply(i, unit)
+        def go():
+            nc.vector.memset(x_shift[:, 0, 0:1], 0.0)
 
-        scalar_unit(1)
-        for i in range(TOKEN_TILES):
-            for unit in last_pass:
-                multiply(i, unit)
+        def add_shift(i, c):
+            cols = slice(c * BANK, (c + 1) * BANK)
+            nc.gpsimd.tensor_tensor(out=x_shift[:, i, cols], in0=x_raw[:, i, cols], in1=shift_all[:, cols], op=ALU.add)
 
-        def add_bias(i):
-            for c in range(HALVES):
-                cols = slice(c * BANK, (c + 1) * BANK)
-                nc.vector.scalar_tensor_tensor(
-                    out=proj[:, i, cols],
-                    in0=acc[i][c][:],
-                    scalar=1.0,
-                    in1=bias_all[:, cols],
-                    op0=ALU.mult,
-                    op1=ALU.add,
-                    accum_out=half_sum[:, i * HALVES + c : i * HALVES + c + 1],
-                )
+        hops = dict(go=go, E=add_shift, rg=regroup, q=quantise, vp=vectors_pe, vo=vectors_out, fh=flip_h, ch=copy_h, qh=quantise_h, mm=multiply)
 
-        def statistics(i):
+        def add_bias(i, c):
+            cols = slice(c * BANK, (c + 1) * BANK)
+            nc.vector.scalar_tensor_tensor(
+                out=proj[:, i, cols],
+                in0=acc[i, c][:],
+                scalar=1.0,
+                in1=bias_all[:, cols],
+                op0=ALU.mult,
+                op1=ALU.add,
+                accum_out=half_sum[:, i * HALVES + c : i * HALVES + c + 1],
+            )
+
+        def mean(i):
             halves = slice(i * HALVES, (i + 1) * HALVES)
             nc.scalar.activation(
                 out=half_mean[:, halves],
@@ -231,6 +246,8 @@ def tile_dcadecoderblock_pb_kernel(
                 scale=-1.0 / FEATURES,
                 accum_out=neg_mean[:, i : i + 1],
             )
+
+        def variance(i):
             nc.scalar.activation(
                 out=squares[:, i, :],
                 in_=proj[:, i, :],
@@ -252,30 +269,23 @@ def tile_dcadecoderblock_pb_kernel(
                 out=scaled[:, i, :],
                 in0=proj[:, i, :],
                 scalar=neg_mean[:, i : i + 1],
-                in1=gain_all,
+                in1=held["spread", 1][:],
                 op0=ALU.add,
                 op1=ALU.mult,
             )
 
-        def finish(i):
-            for c in range(HALVES):
-                cols = slice(c * BANK, (c + 1) * BANK)
-                nc.vector.scalar_tensor_tensor(
-                    out=result[:, i, cols],
-                    in0=scaled[:, i, cols],
-                    scalar=rstd[:, i : i + 1],
-                    in1=x_shift[:, i, cols],
-                    op0=ALU.mult,
-                    op1=ALU.add,
-                )
-                nc.sync.dma_start(out=out_rows[i * P : (i + 1) * P, cols], in_=result[:, i, cols])
+        def finish(i, c):
+            cols = slice(c * BANK, (c + 1) * BANK)
+            nc.vector.scalar_tensor_tensor(
+                out=result[:, i, cols],
+                in0=scaled[:, i, cols],
+                scalar=rstd[:, i : i + 1],
+                in1=x_shift[:, i, cols],
+                op0=ALU.mult,
+                op1=ALU.add,
+            )
+            nc.sync.dma_start(out=out_rows[i * P : (i + 1) * P, cols], in_=result[:, i, cols])
 
-        for step in range(TOKEN_TILES + 2):
-            first, second, third = step, step - 1, step - 2
-            if first < TOKEN_TILES:
-                add_bias(first)
-                statistics(first)
-            if 0 <= second < TOKEN_TILES:
-                centre_and_gain(second)
-            if 0 <= third < TOKEN_TILES:
-                finish(third)
+        hops.update(A=add_bias, mu=mean, var=variance, C=centre_and_gain, D=finish)
+        for op in HEAD + ORDER:
+            hops[op[0]](*op[1:])

@@ -42,11 +42,14 @@ def tile_dcadecoderblock_pb_kernel(
     def both(name, i):
         return [(name, i, 0), (name, i, 1)]
 
-    BANKS = {("spread", 0): 0, ("spread", 2): 1, ("spread", 1): 6}
+    BANKS = {("spread", 0): 0, ("spread", 2): 1, ("spread", 1): 6, "vec_t": 7}
     for i in tiles:
         BANKS["h", i] = 2 + i
         BANKS["acc", i, 0] = (6, 0, 2, 4)[i]
         BANKS["acc", i, 1] = (7, 1, 3, 5)[i]
+    for c in range(HALVES):
+        BANKS["T1", c] = c
+        BANKS["T2", c] = 2 + c
     LOADS = [("w", 0), ("v",), ("w", 1)] + [("h", i) for i in tiles] + [("w", 2), ("w", 3)] + [("x", i) for i in tiles]
     HEAD = (
         [("rg", "V", 0, 0, early), ("rg", "S", 0, early, BANK), ("vp", 0), ("vp", 2), ("rg", "V", 1, 0, early), ("rg", "S", 1, early, BANK)]
@@ -57,10 +60,12 @@ def tile_dcadecoderblock_pb_kernel(
     )
     ORDER = (
         [step for i in tiles for step in both("E", i)]
-        + both("A", 0) + [("mu", 0), ("var", 0), ("vp", 1)]
-        + [step for i in tiles[1:] for step in both("A", i) + [("mu", i), ("var", i)]]
-        + [("C", i) for i in tiles]
-        + [step for i in tiles for step in both("D", i)]
+        + both("A", 0) + [("mu", 0), ("oc", 0), ("var", 0), ("vp", 1), ("vt",), ("vg",)]
+        + both("A", 1) + [("mu", 1), ("var", 1)] + both("T1", 0)
+        + both("A", 2) + [("mu", 2), ("Y", 0, 0)]
+        + both("A", 3) + [("mu", 3), ("Y", 0, 1), ("var", 2), ("var", 3)] + both("T2", 0)
+        + [("C", i) for i in tiles[1:]]
+        + both("Dp", 0) + [step for i in tiles[1:] for step in both("D", i)]
     )
     h_rows = h_attn.flatten_outer_dims()
     x_rows = x.flatten_outer_dims()
@@ -88,12 +93,16 @@ def tile_dcadecoderblock_pb_kernel(
         scaled = keep.tile([P, TOKEN_TILES, FEATURES], F32)
         x_shift = keep.tile([P, TOKEN_TILES, FEATURES], F32)
         shift_all = keep.tile([P, FEATURES], BF16)
+        gain_col = keep.tile([P, BLOCKS], F32)
+        centred = keep.tile([P, FEATURES], F32)
+        turned = keep.tile([P, BLOCKS, P], F32)
         result = keep.tile([P, TOKEN_TILES, FEATURES], F32)
         squares = keep.tile([P, TOKEN_TILES, FEATURES], BF16)
         vec_rows = keep.tile([P, FEATURES], BF16)
         bias_all = keep.tile([P, FEATURES], BF16)
         pick = keep.tile([P, 3 * P], BF16)
         ident = keep.tile([P, P], F32)
+        ident_bf = keep.tile([P, P], BF16)
         eps = keep.tile([P, 1], F32)
         warm = keep.tile([P, 1], F32)
         half_sum = keep.tile([P, TOKEN_TILES * HALVES], F32)
@@ -135,6 +144,7 @@ def tile_dcadecoderblock_pb_kernel(
         nc.vector.memset(pick[2 * QUADRANT : 2 * QUADRANT + 1, 2 * P : 3 * P], 1.0)
         nc.vector.memset(eps[:], EPS)
         make_identity(nc, ident[:])
+        make_identity(nc, ident_bf[:])
         nc.scalar.activation(out=warm[:], in_=eps[:], func=ACT.Abs_reciprocal_sqrt)
 
         def regroup(eng, unit, lo, hi):
@@ -162,6 +172,12 @@ def tile_dcadecoderblock_pb_kernel(
                     stop=True,
                 )
             held["spread", v] = spread
+
+        def vectors_turn():
+            vec_t = bank_tile(BANKS["vec_t"], [P, BLOCKS, P], BF16)
+            for j in range(BLOCKS):
+                nc.tensor.transpose(vec_t[:, j, :], vec_rows[:, j * P : (j + 1) * P], ident_bf[:])
+            held["vec_t"] = vec_t
 
         def vectors_out(v):
             nc.scalar.copy(out=(bias_all if v == 0 else shift_all)[:], in_=held["spread", v][:])
@@ -216,6 +232,47 @@ def tile_dcadecoderblock_pb_kernel(
                 stop=(g == PASSES - 1),
             )
 
+        def gain_column():
+            nc.scalar.copy(out=gain_col[:], in_=held["vec_t"][:, :, QUADRANT])
+
+        def centre_on_scalar(i):
+            nc.scalar.activation(
+                out=centred[:], in_=proj[:, i, :], func=ACT.Identity, bias=neg_mean[:, i : i + 1], scale=1.0
+            )
+
+        def turn(i, c):
+            bank = bank_tile(BANKS["T1", c], [P, BANK_BLOCKS, P], F32)
+            held["T1", c] = bank
+            for b in range(BANK_BLOCKS):
+                j = c * BANK_BLOCKS + b
+                nc.tensor.transpose(bank[:, b, :], centred[:, j * P : (j + 1) * P], ident[:])
+
+        def gain_on_scalar(i, c):
+            for b in range(BANK_BLOCKS):
+                j = c * BANK_BLOCKS + b
+                nc.scalar.activation(
+                    out=turned[:, j, :], in_=held["T1", c][:, b, :], func=ACT.Copy, scale=gain_col[:, j : j + 1]
+                )
+
+        def turn_back(i, c):
+            bank = bank_tile(BANKS["T2", c], [P, BANK], F32)
+            held["T2", c] = bank
+            for b in range(BANK_BLOCKS):
+                j = c * BANK_BLOCKS + b
+                nc.tensor.transpose(bank[:, b * P : (b + 1) * P], turned[:, j, :], ident[:])
+
+        def finish_from_psum(i, c):
+            cols = slice(c * BANK, (c + 1) * BANK)
+            nc.vector.scalar_tensor_tensor(
+                out=result[:, i, cols],
+                in0=held["T2", c][:],
+                scalar=rstd[:, i : i + 1],
+                in1=x_shift[:, i, cols],
+                op0=ALU.mult,
+                op1=ALU.add,
+            )
+            nc.sync.dma_start(out=out_rows[i * P : (i + 1) * P, cols], in_=result[:, i, cols])
+
         def go():
             nc.vector.memset(x_shift[:, 0, 0:1], 0.0)
 
@@ -223,7 +280,7 @@ def tile_dcadecoderblock_pb_kernel(
             cols = slice(c * BANK, (c + 1) * BANK)
             nc.gpsimd.tensor_tensor(out=x_shift[:, i, cols], in0=x_raw[:, i, cols], in1=shift_all[:, cols], op=ALU.add)
 
-        hops = dict(go=go, E=add_shift, rg=regroup, q=quantise, vp=vectors_pe, vo=vectors_out, fh=flip_h, ch=copy_h, qh=quantise_h, mm=multiply)
+        hops = dict(vg=gain_column, oc=centre_on_scalar, T1=turn, Y=gain_on_scalar, T2=turn_back, Dp=finish_from_psum, vt=vectors_turn, go=go, E=add_shift, rg=regroup, q=quantise, vp=vectors_pe, vo=vectors_out, fh=flip_h, ch=copy_h, qh=quantise_h, mm=multiply)
 
         def add_bias(i, c):
             cols = slice(c * BANK, (c + 1) * BANK)

@@ -38,6 +38,7 @@ def tile_dcadecoderblock_pb_kernel(
     nc = tc.nc
     tiles = range(TOKEN_TILES)
     early, late = 320, 256
+    GO_TILE = 1
 
     def both(name, i):
         return [(name, i, 0), (name, i, 1)]
@@ -48,8 +49,8 @@ def tile_dcadecoderblock_pb_kernel(
         BANKS["acc", i, 0] = (6, 0, 2, 4)[i]
         BANKS["acc", i, 1] = (7, 1, 3, 5)[i]
     for c in range(HALVES):
-        BANKS["T1", c] = c
-        BANKS["T2", c] = 2 + c
+        BANKS["T1", 0, c] = c
+        BANKS["T2", 0, c] = 2 + c
     LOADS = [("w", 0), ("v",), ("w", 1)] + [("h", i) for i in tiles] + [("w", 2), ("w", 3)] + [("x", i) for i in tiles]
     HEAD = (
         [("rg", "V", 0, 0, early), ("rg", "S", 0, early, BANK), ("vp", 0), ("vp", 2), ("rg", "V", 1, 0, early), ("rg", "S", 1, early, BANK)]
@@ -59,13 +60,13 @@ def tile_dcadecoderblock_pb_kernel(
         + [("q", 2), ("q", 3), ("go",)] + [("mm", i, u) for i in tiles for u in (2, 3)]
     )
     ORDER = (
-        [step for i in tiles for step in both("E", i)]
-        + both("A", 0) + [("mu", 0), ("oc", 0), ("var", 0), ("vp", 1), ("vt",), ("vg",)]
-        + both("A", 1) + [("mu", 1), ("var", 1)] + both("T1", 0)
-        + both("A", 2) + [("mu", 2), ("Y", 0, 0)]
-        + both("A", 3) + [("mu", 3), ("Y", 0, 1), ("var", 2), ("var", 3)] + both("T2", 0)
+        both("E", 1)
+        + both("A", 0) + [("mu", 0), ("var", 0)] + both("nG", 0) + both("E", 2) + both("E", 3) + [("vp", 1), ("vt",), ("vg2",)]
+        + both("A", 1) + [("mu", 1), ("var", 1)] + both("T1n", 0)
+        + both("A", 2) + [("mu", 2), ("Yn", 0, 0)]
+        + both("A", 3) + [("mu", 3), ("Yn", 0, 1), ("var", 2), ("var", 3)] + both("T2n", 0)
         + [("C", i) for i in tiles[1:]]
-        + both("Dp", 0) + [step for i in tiles[1:] for step in both("D", i)]
+        + both("F", 0) + [step for i in tiles[1:] for step in both("D", i)]
     )
     h_rows = h_attn.flatten_outer_dims()
     x_rows = x.flatten_outer_dims()
@@ -93,9 +94,9 @@ def tile_dcadecoderblock_pb_kernel(
         scaled = keep.tile([P, TOKEN_TILES, FEATURES], F32)
         x_shift = keep.tile([P, TOKEN_TILES, FEATURES], F32)
         shift_all = keep.tile([P, FEATURES], BF16)
-        gain_col = keep.tile([P, BLOCKS], F32)
-        centred = keep.tile([P, FEATURES], F32)
-        turned = keep.tile([P, BLOCKS, P], F32)
+        vec_cols = keep.tile([P, BLOCKS, 2], F32)
+        normed = keep.tile([P, 2, FEATURES], F32)
+        turned2 = keep.tile([P, 2, BLOCKS, P], F32)
         result = keep.tile([P, TOKEN_TILES, FEATURES], F32)
         squares = keep.tile([P, TOKEN_TILES, FEATURES], BF16)
         vec_rows = keep.tile([P, FEATURES], BF16)
@@ -232,55 +233,58 @@ def tile_dcadecoderblock_pb_kernel(
                 stop=(g == PASSES - 1),
             )
 
-        def gain_column():
-            nc.scalar.copy(out=gain_col[:], in_=held["vec_t"][:, :, QUADRANT])
+        def both_columns():
+            nc.scalar.copy(out=vec_cols[:], in_=held["vec_t"][:, :, QUADRANT : 2 * QUADRANT + 1 : QUADRANT])
 
-        def centre_on_scalar(i):
-            nc.scalar.activation(
-                out=centred[:], in_=proj[:, i, :], func=ACT.Identity, bias=neg_mean[:, i : i + 1], scale=1.0
+        def normalise_on_gpsimd(i, c):
+            cols = slice(c * BANK, (c + 1) * BANK)
+            nc.gpsimd.tensor_scalar(
+                out=normed[:, i, cols],
+                in0=proj[:, i, cols],
+                scalar1=neg_mean[:, i : i + 1],
+                scalar2=rstd[:, i : i + 1],
+                op0=ALU.add,
+                op1=ALU.mult,
             )
 
-        def turn(i, c):
-            bank = bank_tile(BANKS["T1", c], [P, BANK_BLOCKS, P], F32)
-            held["T1", c] = bank
+        def turn_n(i, c):
+            bank = bank_tile(BANKS["T1", i, c], [P, BANK_BLOCKS, P], F32)
+            held["T1", i, c] = bank
             for b in range(BANK_BLOCKS):
                 j = c * BANK_BLOCKS + b
-                nc.tensor.transpose(bank[:, b, :], centred[:, j * P : (j + 1) * P], ident[:])
+                nc.tensor.transpose(bank[:, b, :], normed[:, i, j * P : (j + 1) * P], ident[:])
 
-        def gain_on_scalar(i, c):
+        def gain_and_shift(i, c):
             for b in range(BANK_BLOCKS):
                 j = c * BANK_BLOCKS + b
                 nc.scalar.activation(
-                    out=turned[:, j, :], in_=held["T1", c][:, b, :], func=ACT.Copy, scale=gain_col[:, j : j + 1]
+                    out=turned2[:, i, j, :],
+                    in_=held["T1", i, c][:, b, :],
+                    func=ACT.Identity,
+                    bias=vec_cols[:, j, 1:2],
+                    scale=vec_cols[:, j, 0:1],
                 )
 
-        def turn_back(i, c):
-            bank = bank_tile(BANKS["T2", c], [P, BANK], F32)
-            held["T2", c] = bank
+        def turn_back_n(i, c):
+            bank = bank_tile(BANKS["T2", i, c], [P, BANK], F32)
+            held["T2", i, c] = bank
             for b in range(BANK_BLOCKS):
                 j = c * BANK_BLOCKS + b
-                nc.tensor.transpose(bank[:, b * P : (b + 1) * P], turned[:, j, :], ident[:])
+                nc.tensor.transpose(bank[:, b * P : (b + 1) * P], turned2[:, i, j, :], ident[:])
 
-        def finish_from_psum(i, c):
+        def add_x(i, c):
             cols = slice(c * BANK, (c + 1) * BANK)
-            nc.vector.scalar_tensor_tensor(
-                out=result[:, i, cols],
-                in0=held["T2", c][:],
-                scalar=rstd[:, i : i + 1],
-                in1=x_shift[:, i, cols],
-                op0=ALU.mult,
-                op1=ALU.add,
-            )
+            nc.vector.tensor_tensor(out=result[:, i, cols], in0=held["T2", i, c][:], in1=x_raw[:, i, cols], op=ALU.add)
             nc.sync.dma_start(out=out_rows[i * P : (i + 1) * P, cols], in_=result[:, i, cols])
 
         def go():
-            nc.vector.memset(x_shift[:, 0, 0:1], 0.0)
+            nc.vector.memset(x_shift[:, GO_TILE, 0:1], 0.0)
 
         def add_shift(i, c):
             cols = slice(c * BANK, (c + 1) * BANK)
             nc.gpsimd.tensor_tensor(out=x_shift[:, i, cols], in0=x_raw[:, i, cols], in1=shift_all[:, cols], op=ALU.add)
 
-        hops = dict(vg=gain_column, oc=centre_on_scalar, T1=turn, Y=gain_on_scalar, T2=turn_back, Dp=finish_from_psum, vt=vectors_turn, go=go, E=add_shift, rg=regroup, q=quantise, vp=vectors_pe, vo=vectors_out, fh=flip_h, ch=copy_h, qh=quantise_h, mm=multiply)
+        hops = dict(vg2=both_columns, nG=normalise_on_gpsimd, T1n=turn_n, Yn=gain_and_shift, T2n=turn_back_n, F=add_x, vt=vectors_turn, go=go, E=add_shift, rg=regroup, q=quantise, vp=vectors_pe, vo=vectors_out, fh=flip_h, ch=copy_h, qh=quantise_h, mm=multiply)
 
         def add_bias(i, c):
             cols = slice(c * BANK, (c + 1) * BANK)

@@ -25,7 +25,7 @@ PASSES = K // K_PASS
 BANK = 512
 HALVES = FEATURES // BANK
 UNITS = PASSES * HALVES
-RUN = 4
+RUN = 8
 QUADRANT = 32
 BLOCKS = FEATURES // P
 BANK_BLOCKS = BANK // P

@@ -23,12 +23,17 @@ EPS = 1e-5
 TOKEN_TILES = TOKENS // P
 PASSES = K // K_PASS
 BANK = 512
+PSUM_BANKS = 8
 HALVES = FEATURES // BANK
 UNITS = PASSES * HALVES
-RUN = 8
-QUADRANT = 32
 BLOCKS = FEATURES // P
 BANK_BLOCKS = BANK // P
+RUN = 8
+QUADRANT = 32
+BIAS, GAIN, SHIFT = 0, 1, 2
+VECTORS = 3
+VECTOR_SHARE = (320, 320, 256, 256)
+TURNED = 0
 FLOPS = 2 * TOKENS * K * FEATURES
 
 
@@ -36,41 +41,14 @@ def tile_dcadecoderblock_pb_kernel(
     tc, h_attn, x, attn_out_W, attn_out_b, attn_norm_g, attn_norm_b, out
 ):
     nc = tc.nc
-    tiles = range(TOKEN_TILES)
-    early, late = 320, 256
-    GO_TILE = 1
-
-    def both(name, i):
-        return [(name, i, 0), (name, i, 1)]
-
-    BANKS = {("spread", 0): 0, ("spread", 2): 1, ("spread", 1): 6, "vec_t": 7}
-    for i in tiles:
-        BANKS["h", i] = 2 + i
-        BANKS["acc", i, 0] = (6, 0, 2, 4)[i]
-        BANKS["acc", i, 1] = (7, 1, 3, 5)[i]
-    for c in range(HALVES):
-        BANKS["T1", 0, c] = c
-        BANKS["T2", 0, c] = 2 + c
-    LOADS = [("w", 0), ("v",), ("w", 1)] + [("h", i) for i in tiles] + [("w", 2), ("w", 3)] + [("x", i) for i in tiles]
-    HEAD = (
-        [("rg", "V", 0, 0, early), ("rg", "S", 0, early, BANK), ("vp", 0), ("vp", 2), ("rg", "V", 1, 0, early), ("rg", "S", 1, early, BANK)]
-        + [("vo", 0), ("vo", 2), ("q", 0), ("q", 1)] + [("fh", i) for i in tiles] + [("ch", i) for i in tiles]
-        + [step for i in tiles for step in (("qh", i), ("mm", i, 0), ("mm", i, 1))]
-        + [("rg", "S", 2, late, BANK), ("rg", "S", 3, late, BANK), ("rg", "V", 2, 0, late), ("rg", "V", 3, 0, late)]
-        + [("q", 2), ("q", 3), ("go",)] + [("mm", i, u) for i in tiles for u in (2, 3)]
-    )
-    ORDER = (
-        both("E", 1)
-        + both("A", 0) + [("mu", 0), ("var", 0)] + both("nG", 0) + both("E", 2) + both("E", 3) + [("vp", 1), ("vt",), ("vg2",)]
-        + both("A", 1) + [("mu", 1), ("var", 1)] + both("T1n", 0)
-        + both("A", 2) + [("mu", 2), ("Yn", 0, 0)]
-        + both("A", 3) + [("mu", 3), ("Yn", 0, 1), ("var", 2), ("var", 3)] + both("T2n", 0)
-        + [("C", i) for i in tiles[1:]]
-        + both("F", 0) + [step for i in tiles[1:] for step in both("D", i)]
-    )
     h_rows = h_attn.flatten_outer_dims()
     x_rows = x.flatten_outer_dims()
     out_rows = out.flatten_outer_dims()
+    tiles = range(TOKEN_TILES)
+    straight = [i for i in tiles if i != TURNED]
+    halves = range(HALVES)
+    first_pass = range(HALVES)
+    last_pass = range(UNITS - HALVES, UNITS)
 
     with ExitStack() as ctx:
         keep = ctx.enter_context(tc.tile_pool(name="keep", bufs=1))
@@ -78,6 +56,15 @@ def tile_dcadecoderblock_pb_kernel(
 
         def bank_tile(k, shape, dtype):
             return psum.tile(shape, dtype, tag="bank%d" % k, name="bank%d" % k)
+
+        def sums_bank(i, c):
+            return (HALVES * i + c + PSUM_BANKS - HALVES) % PSUM_BANKS
+
+        spread_bank = {BIAS: 0, SHIFT: 1, GAIN: sums_bank(0, 0)}
+        columns_bank = sums_bank(0, 1)
+        h_bank = 2
+        there_bank = [sums_bank(1, c) for c in halves]
+        back_bank = [sums_bank(2, c) for c in halves]
 
         ctx.enter_context(tc.manual_schedule())
 
@@ -95,13 +82,13 @@ def tile_dcadecoderblock_pb_kernel(
         x_shift = keep.tile([P, TOKEN_TILES, FEATURES], F32)
         shift_all = keep.tile([P, FEATURES], BF16)
         vec_cols = keep.tile([P, BLOCKS, 2], F32)
-        normed = keep.tile([P, 2, FEATURES], F32)
-        turned2 = keep.tile([P, 2, BLOCKS, P], F32)
+        normed = keep.tile([P, FEATURES], F32)
+        affine_t = keep.tile([P, BLOCKS, P], F32)
         result = keep.tile([P, TOKEN_TILES, FEATURES], F32)
         squares = keep.tile([P, TOKEN_TILES, FEATURES], BF16)
         vec_rows = keep.tile([P, FEATURES], BF16)
         bias_all = keep.tile([P, FEATURES], BF16)
-        pick = keep.tile([P, 3 * P], BF16)
+        pick = keep.tile([P, VECTORS * P], BF16)
         ident = keep.tile([P, P], F32)
         ident_bf = keep.tile([P, P], BF16)
         eps = keep.tile([P, 1], F32)
@@ -121,39 +108,41 @@ def tile_dcadecoderblock_pb_kernel(
                 ].rearrange("(p t) c -> p t c", t=PACK),
             )
 
-        def load_h(i):
+        nc.vector.memset(vec_rows[:].bitcast(I32), 0)
+        load_weight(first_pass[0])
+        for v, vec in ((BIAS, attn_out_b), (GAIN, attn_norm_g), (SHIFT, attn_norm_b)):
+            row = v * QUADRANT
+            nc.sync.dma_start(
+                out=vec_rows[row : row + 1, :], in_=vec.rearrange("(o c) -> o c", o=1)
+            )
+        load_weight(first_pass[1])
+        for i in tiles:
             nc.sync.dma_start(out=h_raw[:, i * K : (i + 1) * K], in_=h_rows[i * P : (i + 1) * P, :])
-
-        def load_vecs():
-            for v, vec in enumerate((attn_out_b, attn_norm_g, attn_norm_b)):
-                row = v * QUADRANT
-                nc.sync.dma_start(
-                    out=vec_rows[row : row + 1, :], in_=vec.rearrange("(o c) -> o c", o=1)
-                )
-
-        def load_x(i):
+        for unit in last_pass:
+            load_weight(unit)
+        for i in tiles:
             nc.sync.dma_start(out=x_raw[:, i, :], in_=x_rows[i * P : (i + 1) * P, :])
 
-        nc.vector.memset(vec_rows[:].bitcast(I32), 0)
-        loaders = dict(w=load_weight, h=load_h, v=lambda: load_vecs(), x=load_x)
-        for op in LOADS:
-            loaders[op[0]](*op[1:])
-
         nc.vector.memset(pick[:].bitcast(I32), 0)
-        nc.vector.memset(pick[0:1, 0:P], 1.0)
-        nc.vector.memset(pick[QUADRANT : QUADRANT + 1, P : 2 * P], 1.0)
-        nc.vector.memset(pick[2 * QUADRANT : 2 * QUADRANT + 1, 2 * P : 3 * P], 1.0)
+        for v in (BIAS, GAIN, SHIFT):
+            row = v * QUADRANT
+            nc.vector.memset(pick[row : row + 1, v * P : (v + 1) * P], 1.0)
         nc.vector.memset(eps[:], EPS)
         make_identity(nc, ident[:])
         make_identity(nc, ident_bf[:])
         nc.scalar.activation(out=warm[:], in_=eps[:], func=ACT.Abs_reciprocal_sqrt)
 
-        def regroup(eng, unit, lo, hi):
-            copy = nc.vector.tensor_copy if eng == "V" else nc.scalar.copy
+        def regroup(copy, unit, lo, hi):
             copy(
                 out=w_grp[:, unit, lo:hi, :].rearrange("p (c i) t -> p c t i", i=RUN),
                 in_=w_raw[:, unit, :, lo:hi].rearrange("p t (c i) -> p c t i", i=RUN),
             )
+
+        def regroup_on_vector(unit):
+            regroup(nc.vector.tensor_copy, unit, 0, VECTOR_SHARE[unit])
+
+        def regroup_on_scalar(unit):
+            regroup(nc.scalar.copy, unit, VECTOR_SHARE[unit], BANK)
 
         def quantise(unit):
             nc.vector.quantize_mx(
@@ -162,58 +151,48 @@ def tile_dcadecoderblock_pb_kernel(
                 in_=w_grp[:, unit, :, :].rearrange("p c t -> p (c t)"),
             )
 
-        def vectors_pe(v):
-            spread = bank_tile(BANKS["spread", v], [P, FEATURES], BF16)
-            for c in range(HALVES):
+        def spread(v):
+            everywhere = bank_tile(spread_bank[v], [P, FEATURES], BF16)
+            for c in halves:
                 nc.tensor.matmul(
-                    out=spread[:, c * BANK : (c + 1) * BANK],
+                    out=everywhere[:, c * BANK : (c + 1) * BANK],
                     lhsT=pick[:, v * P : (v + 1) * P],
                     rhs=vec_rows[:, c * BANK : (c + 1) * BANK],
                     start=True,
                     stop=True,
                 )
-            held["spread", v] = spread
+            return everywhere
 
-        def vectors_turn():
-            vec_t = bank_tile(BANKS["vec_t"], [P, BLOCKS, P], BF16)
-            for j in range(BLOCKS):
-                nc.tensor.transpose(vec_t[:, j, :], vec_rows[:, j * P : (j + 1) * P], ident_bf[:])
-            held["vec_t"] = vec_t
+        regroup_on_vector(first_pass[0])
+        regroup_on_scalar(first_pass[0])
+        bias_bank = spread(BIAS)
+        shift_bank = spread(SHIFT)
+        regroup_on_vector(first_pass[1])
+        regroup_on_scalar(first_pass[1])
+        nc.scalar.copy(out=bias_all[:], in_=bias_bank[:])
+        nc.scalar.copy(out=shift_all[:], in_=shift_bank[:])
+        for unit in first_pass:
+            quantise(unit)
 
-        def vectors_out(v):
-            nc.scalar.copy(out=(bias_all if v == 0 else shift_all)[:], in_=held["spread", v][:])
-
-        held = {}
         h_words = h_raw[:].bitcast(F32).rearrange(
             "r (i g p u) -> r i g u p", i=TOKEN_TILES, g=PASSES, u=PAIR
         )
         h_grp_words = h_grp[:].bitcast(F32).rearrange(
             "p (i g r u) -> p i g r u", i=TOKEN_TILES, g=PASSES, u=PAIR
         )
-
-        def flip_h(i):
-            flipped = bank_tile(BANKS["h", i], [P, BANK], F32)
+        flipped = []
+        for i in tiles:
+            flipped.append(bank_tile(h_bank + i, [P, BANK], F32))
             for g in range(PASSES):
                 for u in range(PAIR):
                     piece = (g * PAIR + u) * P
                     nc.tensor.transpose(
-                        flipped[:, piece : piece + P], h_words[:, i, g, u, :], ident[:]
+                        flipped[i][:, piece : piece + P], h_words[:, i, g, u, :], ident[:]
                     )
-            held["h", i] = flipped
-
-        def copy_h(i, eng="S"):
-            copy = nc.vector.tensor_copy if eng == "V" else nc.scalar.copy
-            copy(
+        for i in tiles:
+            nc.scalar.copy(
                 out=h_grp_words[:, i],
-                in_=held["h", i][:].rearrange("p (g u r) -> p g r u", g=PASSES, u=PAIR),
-            )
-
-        def quantise_h(i):
-            words = slice(i * PASSES * P, (i + 1) * PASSES * P)
-            nc.vector.quantize_mx(
-                out=h_codes[:, words].bitcast(FP8X4),
-                scales=h_scales[:, words],
-                in_=h_grp[:, i * K : (i + 1) * K],
+                in_=flipped[i][:].rearrange("p (g u r) -> p g r u", g=PASSES, u=PAIR),
             )
 
         acc = {}
@@ -221,7 +200,7 @@ def tile_dcadecoderblock_pb_kernel(
         def multiply(i, unit):
             g, c = divmod(unit, HALVES)
             if g == 0:
-                acc[i, c] = bank_tile(BANKS["acc", i, c], [P, BANK], F32)
+                acc[i, c] = bank_tile(sums_bank(i, c), [P, BANK], F32)
             words = slice((i * PASSES + g) * P, (i * PASSES + g + 1) * P)
             nc.tensor.matmul_mx(
                 out=acc[i, c][:],
@@ -233,82 +212,59 @@ def tile_dcadecoderblock_pb_kernel(
                 stop=(g == PASSES - 1),
             )
 
-        def both_columns():
-            nc.scalar.copy(out=vec_cols[:], in_=held["vec_t"][:, :, QUADRANT : 2 * QUADRANT + 1 : QUADRANT])
-
-        def normalise_on_gpsimd(i, c):
-            cols = slice(c * BANK, (c + 1) * BANK)
-            nc.gpsimd.tensor_scalar(
-                out=normed[:, i, cols],
-                in0=proj[:, i, cols],
-                scalar1=neg_mean[:, i : i + 1],
-                scalar2=rstd[:, i : i + 1],
-                op0=ALU.add,
-                op1=ALU.mult,
+        for i in tiles:
+            words = slice(i * PASSES * P, (i + 1) * PASSES * P)
+            nc.vector.quantize_mx(
+                out=h_codes[:, words].bitcast(FP8X4),
+                scales=h_scales[:, words],
+                in_=h_grp[:, i * K : (i + 1) * K],
             )
+            for unit in first_pass:
+                multiply(i, unit)
 
-        def turn_n(i, c):
-            bank = bank_tile(BANKS["T1", i, c], [P, BANK_BLOCKS, P], F32)
-            held["T1", i, c] = bank
-            for b in range(BANK_BLOCKS):
-                j = c * BANK_BLOCKS + b
-                nc.tensor.transpose(bank[:, b, :], normed[:, i, j * P : (j + 1) * P], ident[:])
+        for unit in last_pass:
+            regroup_on_scalar(unit)
+        for unit in last_pass:
+            regroup_on_vector(unit)
+        for unit in last_pass:
+            quantise(unit)
+        nc.vector.memset(x_shift[:, straight[0], 0:1], 0.0)
+        for i in tiles:
+            for unit in last_pass:
+                multiply(i, unit)
 
-        def gain_and_shift(i, c):
-            for b in range(BANK_BLOCKS):
-                j = c * BANK_BLOCKS + b
-                nc.scalar.activation(
-                    out=turned2[:, i, j, :],
-                    in_=held["T1", i, c][:, b, :],
-                    func=ACT.Identity,
-                    bias=vec_cols[:, j, 1:2],
-                    scale=vec_cols[:, j, 0:1],
+        def half(c):
+            return slice(c * BANK, (c + 1) * BANK)
+
+        def add_shift(i):
+            for c in halves:
+                nc.gpsimd.tensor_tensor(
+                    out=x_shift[:, i, half(c)], in0=x_raw[:, i, half(c)], in1=shift_all[:, half(c)], op=ALU.add
                 )
 
-        def turn_back_n(i, c):
-            bank = bank_tile(BANKS["T2", i, c], [P, BANK], F32)
-            held["T2", i, c] = bank
-            for b in range(BANK_BLOCKS):
-                j = c * BANK_BLOCKS + b
-                nc.tensor.transpose(bank[:, b * P : (b + 1) * P], turned2[:, i, j, :], ident[:])
-
-        def add_x(i, c):
-            cols = slice(c * BANK, (c + 1) * BANK)
-            nc.vector.tensor_tensor(out=result[:, i, cols], in0=held["T2", i, c][:], in1=x_raw[:, i, cols], op=ALU.add)
-            nc.sync.dma_start(out=out_rows[i * P : (i + 1) * P, cols], in_=result[:, i, cols])
-
-        def go():
-            nc.vector.memset(x_shift[:, GO_TILE, 0:1], 0.0)
-
-        def add_shift(i, c):
-            cols = slice(c * BANK, (c + 1) * BANK)
-            nc.gpsimd.tensor_tensor(out=x_shift[:, i, cols], in0=x_raw[:, i, cols], in1=shift_all[:, cols], op=ALU.add)
-
-        hops = dict(vg2=both_columns, nG=normalise_on_gpsimd, T1n=turn_n, Yn=gain_and_shift, T2n=turn_back_n, F=add_x, vt=vectors_turn, go=go, E=add_shift, rg=regroup, q=quantise, vp=vectors_pe, vo=vectors_out, fh=flip_h, ch=copy_h, qh=quantise_h, mm=multiply)
-
-        def add_bias(i, c):
-            cols = slice(c * BANK, (c + 1) * BANK)
-            nc.vector.scalar_tensor_tensor(
-                out=proj[:, i, cols],
-                in0=acc[i, c][:],
-                scalar=1.0,
-                in1=bias_all[:, cols],
-                op0=ALU.mult,
-                op1=ALU.add,
-                accum_out=half_sum[:, i * HALVES + c : i * HALVES + c + 1],
-            )
+        def add_bias(i):
+            for c in halves:
+                nc.vector.scalar_tensor_tensor(
+                    out=proj[:, i, half(c)],
+                    in0=acc[i, c][:],
+                    scalar=1.0,
+                    in1=bias_all[:, half(c)],
+                    op0=ALU.mult,
+                    op1=ALU.add,
+                    accum_out=half_sum[:, i * HALVES + c : i * HALVES + c + 1],
+                )
 
         def mean(i):
-            halves = slice(i * HALVES, (i + 1) * HALVES)
+            both = slice(i * HALVES, (i + 1) * HALVES)
             nc.scalar.activation(
-                out=half_mean[:, halves],
-                in_=half_sum[:, halves],
+                out=half_mean[:, both],
+                in_=half_sum[:, both],
                 func=ACT.Copy,
                 scale=-1.0 / FEATURES,
                 accum_out=neg_mean[:, i : i + 1],
             )
 
-        def variance(i):
+        def deviation(i):
             nc.scalar.activation(
                 out=squares[:, i, :],
                 in_=proj[:, i, :],
@@ -330,23 +286,97 @@ def tile_dcadecoderblock_pb_kernel(
                 out=scaled[:, i, :],
                 in0=proj[:, i, :],
                 scalar=neg_mean[:, i : i + 1],
-                in1=held["spread", 1][:],
+                in1=gain_bank[:],
                 op0=ALU.add,
                 op1=ALU.mult,
             )
 
-        def finish(i, c):
-            cols = slice(c * BANK, (c + 1) * BANK)
+        def finish(i, lo, hi):
             nc.vector.scalar_tensor_tensor(
-                out=result[:, i, cols],
-                in0=scaled[:, i, cols],
+                out=result[:, i, lo:hi],
+                in0=scaled[:, i, lo:hi],
                 scalar=rstd[:, i : i + 1],
-                in1=x_shift[:, i, cols],
+                in1=x_shift[:, i, lo:hi],
                 op0=ALU.mult,
                 op1=ALU.add,
             )
-            nc.sync.dma_start(out=out_rows[i * P : (i + 1) * P, cols], in_=result[:, i, cols])
+            nc.sync.dma_start(out=out_rows[i * P : (i + 1) * P, lo:hi], in_=result[:, i, lo:hi])
 
-        hops.update(A=add_bias, mu=mean, var=variance, C=centre_and_gain, D=finish)
-        for op in HEAD + ORDER:
-            hops[op[0]](*op[1:])
+        def normalise():
+            for c in halves:
+                nc.gpsimd.tensor_scalar(
+                    out=normed[:, half(c)],
+                    in0=proj[:, TURNED, half(c)],
+                    scalar1=neg_mean[:, TURNED : TURNED + 1],
+                    scalar2=rstd[:, TURNED : TURNED + 1],
+                    op0=ALU.add,
+                    op1=ALU.mult,
+                )
+
+        def turn_there(c):
+            there = bank_tile(there_bank[c], [P, BANK_BLOCKS, P], F32)
+            for b in range(BANK_BLOCKS):
+                j = c * BANK_BLOCKS + b
+                nc.tensor.transpose(there[:, b, :], normed[:, j * P : (j + 1) * P], ident[:])
+            return there
+
+        def gain_and_shift(c, there):
+            for b in range(BANK_BLOCKS):
+                j = c * BANK_BLOCKS + b
+                nc.scalar.activation(
+                    out=affine_t[:, j, :],
+                    in_=there[:, b, :],
+                    func=ACT.Identity,
+                    bias=vec_cols[:, j, 1:2],
+                    scale=vec_cols[:, j, 0:1],
+                )
+
+        def turn_back(c):
+            back = bank_tile(back_bank[c], [P, BANK], F32)
+            for b in range(BANK_BLOCKS):
+                j = c * BANK_BLOCKS + b
+                nc.tensor.transpose(back[:, b * P : (b + 1) * P], affine_t[:, j, :], ident[:])
+            return back
+
+        def add_x(c, back):
+            nc.vector.tensor_tensor(
+                out=result[:, TURNED, half(c)], in0=back[:], in1=x_raw[:, TURNED, half(c)], op=ALU.add
+            )
+            nc.sync.dma_start(
+                out=out_rows[TURNED * P : (TURNED + 1) * P, half(c)], in_=result[:, TURNED, half(c)]
+            )
+
+        add_shift(straight[0])
+        add_bias(TURNED)
+        mean(TURNED)
+        deviation(TURNED)
+        normalise()
+        for i in straight[1:]:
+            add_shift(i)
+        gain_bank = spread(GAIN)
+        vec_t = bank_tile(columns_bank, [P, BLOCKS, P], BF16)
+        for j in range(BLOCKS):
+            nc.tensor.transpose(vec_t[:, j, :], vec_rows[:, j * P : (j + 1) * P], ident_bf[:])
+        nc.scalar.copy(
+            out=vec_cols[:], in_=vec_t[:, :, GAIN * QUADRANT : SHIFT * QUADRANT + 1 : QUADRANT]
+        )
+        add_bias(straight[0])
+        mean(straight[0])
+        deviation(straight[0])
+        there = [turn_there(c) for c in halves]
+        add_bias(straight[1])
+        mean(straight[1])
+        gain_and_shift(0, there[0])
+        add_bias(straight[2])
+        mean(straight[2])
+        gain_and_shift(1, there[1])
+        deviation(straight[1])
+        deviation(straight[2])
+        back = [turn_back(c) for c in halves]
+        for i in straight:
+            centre_and_gain(i)
+        for c in halves:
+            add_x(c, back[c])
+        for i in straight:
+            for lo, hi in ((0, BANK), (BANK, FEATURES)):
+                finish(i, lo, hi)

@@ -226,9 +226,9 @@ def tile_dcadecoderblock_pb_kernel(
             regroup_on_scalar(unit)
         for unit in last_pass:
             regroup_on_vector(unit)
-        for unit in last_pass:
-            quantise(unit)
+        quantise(last_pass[0])
         nc.vector.memset(x_shift[:, straight[0], 0:1], 0.0)
+        quantise(last_pass[1])
         for i in tiles:
             for unit in last_pass:
                 multiply(i, unit)
@@ -237,10 +237,7 @@ def tile_dcadecoderblock_pb_kernel(
             return slice(c * BANK, (c + 1) * BANK)
 
         def add_shift(i):
-            for c in halves:
-                nc.gpsimd.tensor_tensor(
-                    out=x_shift[:, i, half(c)], in0=x_raw[:, i, half(c)], in1=shift_all[:, half(c)], op=ALU.add
-                )
+            nc.gpsimd.tensor_tensor(out=x_shift[:, i, :], in0=x_raw[:, i, :], in1=shift_all[:], op=ALU.add)
 
         def add_bias(i):
             for c in halves:
@@ -303,15 +300,14 @@ def tile_dcadecoderblock_pb_kernel(
             nc.sync.dma_start(out=out_rows[i * P : (i + 1) * P, lo:hi], in_=result[:, i, lo:hi])
 
         def normalise():
-            for c in halves:
-                nc.gpsimd.tensor_scalar(
-                    out=normed[:, half(c)],
-                    in0=proj[:, TURNED, half(c)],
-                    scalar1=neg_mean[:, TURNED : TURNED + 1],
-                    scalar2=rstd[:, TURNED : TURNED + 1],
-                    op0=ALU.add,
-                    op1=ALU.mult,
-                )
+            nc.gpsimd.tensor_scalar(
+                out=normed[:],
+                in0=proj[:, TURNED, :],
+                scalar1=neg_mean[:, TURNED : TURNED + 1],
+                scalar2=rstd[:, TURNED : TURNED + 1],
+                op0=ALU.add,
+                op1=ALU.mult,
+            )
 
         def turn_there(c):
             there = bank_tile(there_bank[c], [P, BANK_BLOCKS, P], F32)

@@ -32,7 +32,7 @@ RUN = 8
 QUADRANT = 32
 BIAS, GAIN, SHIFT = 0, 1, 2
 VECTORS = 3
-VECTOR_SHARE = (320, 320, 256, 256)
+VECTOR_SHARE = (320, 320, 320, 320)
 TURNED = 0
 FLOPS = 2 * TOKENS * K * FEATURES
 
@@ -45,7 +45,6 @@ def tile_dcadecoderblock_pb_kernel(
     x_rows = x.flatten_outer_dims()
     out_rows = out.flatten_outer_dims()
     tiles = range(TOKEN_TILES)
-    straight = [i for i in tiles if i != TURNED]
     halves = range(HALVES)
     first_pass = range(HALVES)
     last_pass = range(UNITS - HALVES, UNITS)
@@ -60,11 +59,15 @@ def tile_dcadecoderblock_pb_kernel(
         def sums_bank(i, c):
             return (HALVES * i + c + PSUM_BANKS - HALVES) % PSUM_BANKS
 
-        spread_bank = {BIAS: 0, SHIFT: 1, GAIN: sums_bank(0, 0)}
-        columns_bank = sums_bank(0, 1)
-        h_bank = 2
-        there_bank = [sums_bank(1, c) for c in halves]
-        back_bank = [sums_bank(2, c) for c in halves]
+        columns_bank = sums_bank(3, 0)
+        spread_bank = {BIAS: sums_bank(3, 1), GAIN: sums_bank(0, 0)}
+        h_bank = 0
+        turned_bank = (sums_bank(0, 1), sums_bank(1, 0))
+        shifted_bank = {
+            1: (sums_bank(1, 1), sums_bank(2, 0)),
+            2: (sums_bank(2, 1), sums_bank(3, 0)),
+            3: (sums_bank(3, 1), spread_bank[GAIN]),
+        }
 
         ctx.enter_context(tc.manual_schedule())
 
@@ -79,22 +82,29 @@ def tile_dcadecoderblock_pb_kernel(
         x_raw = keep.tile([P, TOKEN_TILES, FEATURES], BF16)
         proj = keep.tile([P, TOKEN_TILES, FEATURES], F32)
         scaled = keep.tile([P, TOKEN_TILES, FEATURES], F32)
-        x_shift = keep.tile([P, TOKEN_TILES, FEATURES], F32)
-        shift_all = keep.tile([P, FEATURES], BF16)
-        vec_cols = keep.tile([P, BLOCKS, 2], F32)
+        vec_cols = keep.tile([P, BLOCKS, VECTORS], F32)
+        vec_cols_bf = keep.tile([P, BLOCKS, VECTORS], BF16)
         normed = keep.tile([P, FEATURES], F32)
         affine_t = keep.tile([P, BLOCKS, P], F32)
         result = keep.tile([P, TOKEN_TILES, FEATURES], F32)
         squares = keep.tile([P, TOKEN_TILES, FEATURES], BF16)
         vec_rows = keep.tile([P, FEATURES], BF16)
         bias_all = keep.tile([P, FEATURES], BF16)
-        pick = keep.tile([P, VECTORS * P], BF16)
         ident = keep.tile([P, P], F32)
         ident_bf = keep.tile([P, P], BF16)
         eps = keep.tile([P, 1], F32)
         warm = keep.tile([P, 1], F32)
         half_sum = keep.tile([P, TOKEN_TILES * HALVES], F32)
         half_mean = keep.tile([P, TOKEN_TILES * HALVES], F32)
+        bias_sums = keep.tile([P, BLOCKS], F32)
+        neg_bias = keep.tile([P, 1], F32)
+        ones = keep.tile([P, P], BF16)
+        gain_all = keep.tile([P, FEATURES], BF16)
+        unread = keep.tile([P, FEATURES], BF16)
+        zeros = keep.tile([P, PACK * BANK], BF16, align_bytes=64)
+        zero_codes = keep.tile([P, BANK], U32, align_bytes=64)
+        zero_scales = keep.tile([P, BANK], U8, align_bytes=64)
+        centred = keep.tile([P, TOKEN_TILES, FEATURES], F32)
         neg_mean = keep.tile([P, TOKEN_TILES], F32)
         sq_sum = keep.tile([P, TOKEN_TILES], F32)
         rstd = keep.tile([P, TOKEN_TILES], F32)
@@ -108,26 +118,35 @@ def tile_dcadecoderblock_pb_kernel(
                 ].rearrange("(p t) c -> p t c", t=PACK),
             )
 
-        nc.vector.memset(vec_rows[:].bitcast(I32), 0)
-        load_weight(first_pass[0])
-        for v, vec in ((BIAS, attn_out_b), (GAIN, attn_norm_g), (SHIFT, attn_norm_b)):
-            row = v * QUADRANT
-            nc.sync.dma_start(
-                out=vec_rows[row : row + 1, :], in_=vec.rearrange("(o c) -> o c", o=1)
-            )
-        load_weight(first_pass[1])
-        for i in tiles:
+        def load_vectors():
+            for v, vec in ((BIAS, attn_out_b), (GAIN, attn_norm_g), (SHIFT, attn_norm_b)):
+                row = v * QUADRANT
+                nc.sync.dma_start(
+                    out=vec_rows[row : row + 1, :], in_=vec.rearrange("(o c) -> o c", o=1)
+                )
+
+        def load_tokens(i):
             nc.sync.dma_start(out=h_raw[:, i * K : (i + 1) * K], in_=h_rows[i * P : (i + 1) * P, :])
-        for unit in last_pass:
-            load_weight(unit)
-        for i in tiles:
+
+        def load_residual(i):
             nc.sync.dma_start(out=x_raw[:, i, :], in_=x_rows[i * P : (i + 1) * P, :])
 
-        nc.vector.memset(pick[:].bitcast(I32), 0)
-        for v in (BIAS, GAIN, SHIFT):
-            row = v * QUADRANT
-            nc.vector.memset(pick[row : row + 1, v * P : (v + 1) * P], 1.0)
+        nc.vector.memset(vec_rows[:].bitcast(I32), 0)
+        load_weight(0)
+        load_vectors()
+        load_weight(1)
+        load_tokens(0)
+        load_tokens(1)
+        load_tokens(2)
+        load_tokens(3)
+        load_weight(2)
+        load_weight(3)
+        load_residual(0)
+        load_residual(1)
+        load_residual(2)
+        load_residual(3)
         nc.vector.memset(eps[:], EPS)
+        nc.vector.memset(ones[:], 1.0)
         make_identity(nc, ident[:])
         make_identity(nc, ident_bf[:])
         nc.scalar.activation(out=warm[:], in_=eps[:], func=ACT.Abs_reciprocal_sqrt)
@@ -153,26 +172,13 @@ def tile_dcadecoderblock_pb_kernel(
 
         def spread(v):
             everywhere = bank_tile(spread_bank[v], [P, FEATURES], BF16)
-            for c in halves:
-                nc.tensor.matmul(
-                    out=everywhere[:, c * BANK : (c + 1) * BANK],
-                    lhsT=pick[:, v * P : (v + 1) * P],
-                    rhs=vec_rows[:, c * BANK : (c + 1) * BANK],
-                    start=True,
-                    stop=True,
+            for j in range(BLOCKS):
+                nc.tensor.transpose(
+                    everywhere[:, j * P : (j + 1) * P],
+                    vec_cols_bf[:, j, v : v + 1].to_broadcast([P, P]),
+                    ident_bf[:],
                 )
             return everywhere
-
-        regroup_on_vector(first_pass[0])
-        regroup_on_scalar(first_pass[0])
-        bias_bank = spread(BIAS)
-        shift_bank = spread(SHIFT)
-        regroup_on_vector(first_pass[1])
-        regroup_on_scalar(first_pass[1])
-        nc.scalar.copy(out=bias_all[:], in_=bias_bank[:])
-        nc.scalar.copy(out=shift_all[:], in_=shift_bank[:])
-        for unit in first_pass:
-            quantise(unit)
 
         h_words = h_raw[:].bitcast(F32).rearrange(
             "r (i g p u) -> r i g u p", i=TOKEN_TILES, g=PASSES, u=PAIR
@@ -180,19 +186,42 @@ def tile_dcadecoderblock_pb_kernel(
         h_grp_words = h_grp[:].bitcast(F32).rearrange(
             "p (i g r u) -> p i g r u", i=TOKEN_TILES, g=PASSES, u=PAIR
         )
-        flipped = []
-        for i in tiles:
-            flipped.append(bank_tile(h_bank + i, [P, BANK], F32))
+        flipped = {}
+
+        def flip(i):
+            flipped[i] = bank_tile(h_bank + i, [P, BANK], F32)
             for g in range(PASSES):
                 for u in range(PAIR):
                     piece = (g * PAIR + u) * P
                     nc.tensor.transpose(
                         flipped[i][:, piece : piece + P], h_words[:, i, g, u, :], ident[:]
                     )
-        for i in tiles:
-            nc.scalar.copy(
+
+        def warm_up(passes):
+            for k in range(passes):
+                idle = bank_tile(sums_bank(0, 1), [P, BANK], F32)
+                nc.tensor.matmul_mx(
+                    out=idle[:],
+                    lhsT=zero_codes[:, 0:P].bitcast(FP8X4),
+                    lhsT_scale=zero_scales[:, 0:P],
+                    rhs=zero_codes[:].bitcast(FP8X4),
+                    rhs_scale=zero_scales[:],
+                    start=True,
+                    stop=True,
+                )
+
+        def collect(copy, i):
+            copy(
                 out=h_grp_words[:, i],
                 in_=flipped[i][:].rearrange("p (g u r) -> p g r u", g=PASSES, u=PAIR),
+            )
+
+        def quantise_tokens(i):
+            words = slice(i * PASSES * P, (i + 1) * PASSES * P)
+            nc.vector.quantize_mx(
+                out=h_codes[:, words].bitcast(FP8X4),
+                scales=h_scales[:, words],
+                in_=h_grp[:, i * K : (i + 1) * K],
             )
 
         acc = {}
@@ -212,32 +241,27 @@ def tile_dcadecoderblock_pb_kernel(
                 stop=(g == PASSES - 1),
             )
 
-        for i in tiles:
-            words = slice(i * PASSES * P, (i + 1) * PASSES * P)
-            nc.vector.quantize_mx(
-                out=h_codes[:, words].bitcast(FP8X4),
-                scales=h_scales[:, words],
-                in_=h_grp[:, i * K : (i + 1) * K],
-            )
-            for unit in first_pass:
-                multiply(i, unit)
-
-        for unit in last_pass:
-            regroup_on_scalar(unit)
-        for unit in last_pass:
-            regroup_on_vector(unit)
-        quantise(last_pass[0])
-        nc.vector.memset(x_shift[:, straight[0], 0:1], 0.0)
-        quantise(last_pass[1])
-        for i in tiles:
-            for unit in last_pass:
-                multiply(i, unit)
-
         def half(c):
             return slice(c * BANK, (c + 1) * BANK)
 
+        shifted = {}
+
         def add_shift(i):
-            nc.gpsimd.tensor_tensor(out=x_shift[:, i, :], in0=x_raw[:, i, :], in1=shift_all[:], op=ALU.add)
+            for c in halves:
+                shifted[i, c] = bank_tile(shifted_bank[i][c], [P, BANK], F32)
+                nc.tensor.matmul(
+                    out=shifted[i, c][:], lhsT=ident_bf[:], rhs=x_raw[:, i, half(c)], start=True, stop=False
+                )
+                for b in range(BANK_BLOCKS):
+                    j = c * BANK_BLOCKS + b
+                    nc.tensor.matmul(
+                        out=shifted[i, c][:, b * P : (b + 1) * P],
+                        lhsT=vec_cols[:, j, SHIFT : SHIFT + 1].to_broadcast([P, P]),
+                        rhs=ident[:],
+                        is_transpose=True,
+                        start=False,
+                        stop=(b == BANK_BLOCKS - 1),
+                    )
 
         def add_bias(i):
             for c in halves:
@@ -260,6 +284,64 @@ def tile_dcadecoderblock_pb_kernel(
                 scale=-1.0 / FEATURES,
                 accum_out=neg_mean[:, i : i + 1],
             )
+
+        def mean_of_sums(i):
+            for c in halves:
+                nc.scalar.activation(
+                    out=unread[:, half(c)],
+                    in_=acc[i, c][:],
+                    func=ACT.Copy,
+                    scale=-1.0 / FEATURES,
+                    accum_out=half_sum[:, i * HALVES + c : i * HALVES + c + 1],
+                )
+            both = slice(i * HALVES, (i + 1) * HALVES)
+            nc.scalar.activation(
+                out=half_mean[:, both],
+                in_=half_sum[:, both],
+                func=ACT.Identity,
+                bias=neg_bias[:],
+                scale=1.0,
+                accum_out=neg_mean[:, i : i + 1],
+            )
+
+        def add_bias_centred(i):
+            for c in halves:
+                nc.vector.scalar_tensor_tensor(
+                    out=proj[:, i, half(c)],
+                    in0=acc[i, c][:],
+                    scalar=neg_mean[:, i : i + 1],
+                    in1=bias_all[:, half(c)],
+                    op0=ALU.add,
+                    op1=ALU.add,
+                )
+
+        def deviation_centred(i):
+            nc.scalar.activation(
+                out=squares[:, i, :],
+                in_=proj[:, i, :],
+                func=ACT.Square,
+                accum_out=sq_sum[:, i : i + 1],
+            )
+            nc.scalar.activation(
+                out=rstd[:, i : i + 1],
+                in_=sq_sum[:, i : i + 1],
+                func=ACT.Abs_reciprocal_sqrt,
+                bias=eps[:],
+                scale=1.0 / FEATURES,
+            )
+
+        def centre_on_gpsimd(i):
+            nc.gpsimd.tensor_scalar(
+                out=centred[:, i, :],
+                in0=proj[:, i, :],
+                scalar1=neg_mean[:, i : i + 1],
+                scalar2=1.0,
+                op0=ALU.add,
+                op1=ALU.mult,
+            )
+
+        def gain_on_gpsimd(i, source):
+            nc.gpsimd.tensor_tensor(out=scaled[:, i, :], in0=source[:, i, :], in1=gain_all[:], op=ALU.mult)
 
         def deviation(i):
             nc.scalar.activation(
@@ -288,16 +370,17 @@ def tile_dcadecoderblock_pb_kernel(
                 op1=ALU.mult,
             )
 
-        def finish(i, lo, hi):
-            nc.vector.scalar_tensor_tensor(
-                out=result[:, i, lo:hi],
-                in0=scaled[:, i, lo:hi],
-                scalar=rstd[:, i : i + 1],
-                in1=x_shift[:, i, lo:hi],
-                op0=ALU.mult,
-                op1=ALU.add,
-            )
-            nc.sync.dma_start(out=out_rows[i * P : (i + 1) * P, lo:hi], in_=result[:, i, lo:hi])
+        def finish(i):
+            for c in halves:
+                nc.vector.scalar_tensor_tensor(
+                    out=result[:, i, half(c)],
+                    in0=scaled[:, i, half(c)],
+                    scalar=rstd[:, i : i + 1],
+                    in1=shifted[i, c][:],
+                    op0=ALU.mult,
+                    op1=ALU.add,
+                )
+                nc.sync.dma_start(out=out_rows[i * P : (i + 1) * P, half(c)], in_=result[:, i, half(c)])
 
         def normalise():
             nc.gpsimd.tensor_scalar(
@@ -310,7 +393,7 @@ def tile_dcadecoderblock_pb_kernel(
             )
 
         def turn_there(c):
-            there = bank_tile(there_bank[c], [P, BANK_BLOCKS, P], F32)
+            there = bank_tile(turned_bank[c], [P, BANK_BLOCKS, P], F32)
             for b in range(BANK_BLOCKS):
                 j = c * BANK_BLOCKS + b
                 nc.tensor.transpose(there[:, b, :], normed[:, j * P : (j + 1) * P], ident[:])
@@ -323,12 +406,12 @@ def tile_dcadecoderblock_pb_kernel(
                     out=affine_t[:, j, :],
                     in_=there[:, b, :],
                     func=ACT.Identity,
-                    bias=vec_cols[:, j, 1:2],
-                    scale=vec_cols[:, j, 0:1],
+                    bias=vec_cols[:, j, SHIFT : SHIFT + 1],
+                    scale=vec_cols[:, j, GAIN : GAIN + 1],
                 )
 
         def turn_back(c):
-            back = bank_tile(back_bank[c], [P, BANK], F32)
+            back = bank_tile(turned_bank[c], [P, BANK], F32)
             for b in range(BANK_BLOCKS):
                 j = c * BANK_BLOCKS + b
                 nc.tensor.transpose(back[:, b * P : (b + 1) * P], affine_t[:, j, :], ident[:])
@@ -342,37 +425,90 @@ def tile_dcadecoderblock_pb_kernel(
                 out=out_rows[TURNED * P : (TURNED + 1) * P, half(c)], in_=result[:, TURNED, half(c)]
             )
 
-        add_shift(straight[0])
-        add_bias(TURNED)
-        mean(TURNED)
-        deviation(TURNED)
-        normalise()
-        for i in straight[1:]:
-            add_shift(i)
-        gain_bank = spread(GAIN)
+        regroup_on_vector(0)
+        regroup_on_scalar(0)
         vec_t = bank_tile(columns_bank, [P, BLOCKS, P], BF16)
         for j in range(BLOCKS):
             nc.tensor.transpose(vec_t[:, j, :], vec_rows[:, j * P : (j + 1) * P], ident_bf[:])
-        nc.scalar.copy(
-            out=vec_cols[:], in_=vec_t[:, :, GAIN * QUADRANT : SHIFT * QUADRANT + 1 : QUADRANT]
+        for cols in (vec_cols_bf, vec_cols):
+            nc.scalar.copy(out=cols[:], in_=vec_t[:, :, 0 : SHIFT * QUADRANT + 1 : QUADRANT])
+        block_sums = bank_tile(columns_bank, [P, BLOCKS], F32)
+        nc.tensor.matmul(out=block_sums[:], lhsT=ones[:], rhs=vec_cols_bf[:, :, BIAS], start=True, stop=True)
+        regroup_on_vector(1)
+        regroup_on_scalar(1)
+        quantise(0)
+        quantise(1)
+        flip(0)
+        flip(1)
+        flip(2)
+        flip(3)
+        collect(nc.scalar.copy, 0)
+        collect(nc.scalar.copy, 1)
+        collect(nc.scalar.copy, 2)
+        collect(nc.scalar.copy, 3)
+        nc.scalar.activation(
+            out=bias_sums[:],
+            in_=block_sums[:],
+            func=ACT.Copy,
+            scale=-1.0 / (HALVES * FEATURES),
+            accum_out=neg_bias[:],
         )
-        add_bias(straight[0])
-        mean(straight[0])
-        deviation(straight[0])
+        quantise_tokens(0)
+        multiply(0, 0)
+        multiply(0, 1)
+        quantise_tokens(1)
+        multiply(1, 0)
+        multiply(1, 1)
+        bias_bank = spread(BIAS)
+        regroup_on_vector(2)
+        regroup_on_scalar(2)
+        quantise_tokens(2)
+        multiply(2, 0)
+        multiply(2, 1)
+        quantise_tokens(3)
+        regroup_on_scalar(3)
+        regroup_on_vector(3)
+        nc.scalar.copy(out=bias_all[:], in_=bias_bank[:])
+        quantise(2)
+        multiply(0, 2)
+        multiply(1, 2)
+        multiply(2, 2)
+        quantise(3)
+        multiply(0, 3)
+        multiply(1, 3)
+        multiply(2, 3)
+        multiply(3, 0)
+        multiply(3, 1)
+        multiply(3, 2)
+        multiply(3, 3)
+        mean_of_sums(1)
+        add_bias(0)
+        mean(0)
+        deviation(0)
+        normalise()
+        gain_bank = spread(GAIN)
+        nc.scalar.copy(out=gain_all[:], in_=gain_bank[:])
+        add_bias_centred(1)
+        gain_on_gpsimd(1, proj)
+        deviation_centred(1)
+        add_bias(2)
+        mean(2)
+        add_bias(3)
+        mean(3)
+        centre_on_gpsimd(3)
+        gain_on_gpsimd(3, centred)
         there = [turn_there(c) for c in halves]
-        add_bias(straight[1])
-        mean(straight[1])
+        add_shift(1)
+        add_shift(2)
+        deviation(2)
         gain_and_shift(0, there[0])
-        add_bias(straight[2])
-        mean(straight[2])
         gain_and_shift(1, there[1])
-        deviation(straight[1])
-        deviation(straight[2])
+        deviation(3)
         back = [turn_back(c) for c in halves]
-        for i in straight:
-            centre_and_gain(i)
+        centre_and_gain(2)
+        add_shift(3)
+        finish(1)
+        finish(2)
         for c in halves:
             add_x(c, back[c])
-        for i in straight:
-            for lo, hi in ((0, BANK), (BANK, FEATURES)):
-                finish(i, lo, hi)
+        finish(3)

@@ -64,9 +64,9 @@ def tile_dcadecoderblock_pb_kernel(
         h_bank = 0
         turned_bank = (sums_bank(0, 1), sums_bank(1, 0))
         shifted_bank = {
-            1: (sums_bank(1, 1), sums_bank(2, 0)),
-            2: (sums_bank(2, 1), sums_bank(3, 0)),
-            3: (sums_bank(3, 1), spread_bank[GAIN]),
+            1: (sums_bank(1, 1), spread_bank[GAIN]),
+            2: (sums_bank(2, 0), sums_bank(2, 1)),
+            3: (sums_bank(3, 0), sums_bank(3, 1)),
         }
 
         ctx.enter_context(tc.manual_schedule())
@@ -101,9 +101,6 @@ def tile_dcadecoderblock_pb_kernel(
         ones = keep.tile([P, P], BF16)
         gain_all = keep.tile([P, FEATURES], BF16)
         unread = keep.tile([P, FEATURES], BF16)
-        zeros = keep.tile([P, PACK * BANK], BF16, align_bytes=64)
-        zero_codes = keep.tile([P, BANK], U32, align_bytes=64)
-        zero_scales = keep.tile([P, BANK], U8, align_bytes=64)
         centred = keep.tile([P, TOKEN_TILES, FEATURES], F32)
         neg_mean = keep.tile([P, TOKEN_TILES], F32)
         sq_sum = keep.tile([P, TOKEN_TILES], F32)
@@ -197,19 +194,6 @@ def tile_dcadecoderblock_pb_kernel(
                         flipped[i][:, piece : piece + P], h_words[:, i, g, u, :], ident[:]
                     )
 
-        def warm_up(passes):
-            for k in range(passes):
-                idle = bank_tile(sums_bank(0, 1), [P, BANK], F32)
-                nc.tensor.matmul_mx(
-                    out=idle[:],
-                    lhsT=zero_codes[:, 0:P].bitcast(FP8X4),
-                    lhsT_scale=zero_scales[:, 0:P],
-                    rhs=zero_codes[:].bitcast(FP8X4),
-                    rhs_scale=zero_scales[:],
-                    start=True,
-                    stop=True,
-                )
-
         def collect(copy, i):
             copy(
                 out=h_grp_words[:, i],
@@ -263,17 +247,16 @@ def tile_dcadecoderblock_pb_kernel(
                         stop=(b == BANK_BLOCKS - 1),
                     )
 
-        def add_bias(i):
-            for c in halves:
-                nc.vector.scalar_tensor_tensor(
-                    out=proj[:, i, half(c)],
-                    in0=acc[i, c][:],
-                    scalar=1.0,
-                    in1=bias_all[:, half(c)],
-                    op0=ALU.mult,
-                    op1=ALU.add,
-                    accum_out=half_sum[:, i * HALVES + c : i * HALVES + c + 1],
-                )
+        def add_bias(i, c):
+            nc.vector.scalar_tensor_tensor(
+                out=proj[:, i, half(c)],
+                in0=acc[i, c][:],
+                scalar=1.0,
+                in1=bias_all[:, half(c)],
+                op0=ALU.mult,
+                op1=ALU.add,
+                accum_out=half_sum[:, i * HALVES + c : i * HALVES + c + 1],
+            )
 
         def mean(i):
             both = slice(i * HALVES, (i + 1) * HALVES)
@@ -304,16 +287,15 @@ def tile_dcadecoderblock_pb_kernel(
                 accum_out=neg_mean[:, i : i + 1],
             )
 
-        def add_bias_centred(i):
-            for c in halves:
-                nc.vector.scalar_tensor_tensor(
-                    out=proj[:, i, half(c)],
-                    in0=acc[i, c][:],
-                    scalar=neg_mean[:, i : i + 1],
-                    in1=bias_all[:, half(c)],
-                    op0=ALU.add,
-                    op1=ALU.add,
-                )
+        def add_bias_centred(i, c):
+            nc.vector.scalar_tensor_tensor(
+                out=proj[:, i, half(c)],
+                in0=acc[i, c][:],
+                scalar=neg_mean[:, i : i + 1],
+                in1=bias_all[:, half(c)],
+                op0=ALU.add,
+                op1=ALU.add,
+            )
 
         def deviation_centred(i):
             nc.scalar.activation(
@@ -330,18 +312,29 @@ def tile_dcadecoderblock_pb_kernel(
                 scale=1.0 / FEATURES,
             )
 
-        def centre_on_gpsimd(i):
-            nc.gpsimd.tensor_scalar(
+        def centre_on_scalar(i):
+            nc.scalar.activation(
                 out=centred[:, i, :],
-                in0=proj[:, i, :],
+                in_=proj[:, i, :],
+                func=ACT.Identity,
+                bias=neg_mean[:, i : i + 1],
+                scale=1.0,
+            )
+
+        def centre_on_gpsimd(i, lo=0, hi=FEATURES):
+            nc.gpsimd.tensor_scalar(
+                out=centred[:, i, lo:hi],
+                in0=proj[:, i, lo:hi],
                 scalar1=neg_mean[:, i : i + 1],
                 scalar2=1.0,
                 op0=ALU.add,
                 op1=ALU.mult,
             )
 
-        def gain_on_gpsimd(i, source):
-            nc.gpsimd.tensor_tensor(out=scaled[:, i, :], in0=source[:, i, :], in1=gain_all[:], op=ALU.mult)
+        def gain_on_gpsimd(i, source, lo=0, hi=FEATURES):
+            nc.gpsimd.tensor_tensor(
+                out=scaled[:, i, lo:hi], in0=source[:, i, lo:hi], in1=gain_all[:, lo:hi], op=ALU.mult
+            )
 
         def deviation(i):
             nc.scalar.activation(
@@ -360,12 +353,12 @@ def tile_dcadecoderblock_pb_kernel(
                 scale=1.0 / FEATURES,
             )
 
-        def centre_and_gain(i):
+        def centre_and_gain(i, lo=0, hi=FEATURES):
             nc.vector.scalar_tensor_tensor(
-                out=scaled[:, i, :],
-                in0=proj[:, i, :],
+                out=scaled[:, i, lo:hi],
+                in0=proj[:, i, lo:hi],
                 scalar=neg_mean[:, i : i + 1],
-                in1=gain_bank[:],
+                in1=gain_bank[:, lo:hi],
                 op0=ALU.add,
                 op1=ALU.mult,
             )
@@ -482,33 +475,38 @@ def tile_dcadecoderblock_pb_kernel(
         multiply(3, 2)
         multiply(3, 3)
         mean_of_sums(1)
-        add_bias(0)
+        for c in halves:
+            add_bias(0, c)
         mean(0)
         deviation(0)
+        nc.sync.dma_start(out=gain_all[:], in_=attn_norm_g.partition_broadcast(P))
         normalise()
         gain_bank = spread(GAIN)
-        nc.scalar.copy(out=gain_all[:], in_=gain_bank[:])
-        add_bias_centred(1)
+        for c in halves:
+            add_bias(2, c)
+        add_shift(2)
+        for c in halves:
+            add_bias_centred(1, c)
         gain_on_gpsimd(1, proj)
-        deviation_centred(1)
-        add_bias(2)
         mean(2)
-        add_bias(3)
-        mean(3)
-        centre_on_gpsimd(3)
-        gain_on_gpsimd(3, centred)
+        mean_of_sums(3)
+        centre_and_gain(2)
+        for c in halves:
+            add_bias_centred(3, c)
+        gain_on_gpsimd(3, proj)
+        deviation(2)
         there = [turn_there(c) for c in halves]
         add_shift(1)
-        add_shift(2)
-        deviation(2)
+        deviation_centred(1)
         gain_and_shift(0, there[0])
+        back = {}
+        back[0] = turn_back(0)
         gain_and_shift(1, there[1])
-        deviation(3)
-        back = [turn_back(c) for c in halves]
-        centre_and_gain(2)
+        back[1] = turn_back(1)
+        deviation_centred(3)
         add_shift(3)
-        finish(1)
         finish(2)
+        finish(1)
         for c in halves:
             add_x(c, back[c])
         finish(3)

@@ -88,7 +88,7 @@ def tile_dcadecoderblock_pb_kernel(
         affine_t = keep.tile([P, BLOCKS, P], F32)
         result = keep.tile([P, TOKEN_TILES, FEATURES], F32)
         squares = keep.tile([P, TOKEN_TILES, FEATURES], BF16)
-        vec_rows = keep.tile([P, FEATURES], BF16)
+        vec_rows = keep.tile([P, FEATURES], BF16, align_bytes=64)
         bias_all = keep.tile([P, FEATURES], BF16)
         ident = keep.tile([P, P], F32)
         ident_bf = keep.tile([P, P], BF16)
@@ -101,6 +101,8 @@ def tile_dcadecoderblock_pb_kernel(
         ones = keep.tile([P, P], BF16)
         gain_all = keep.tile([P, FEATURES], BF16)
         unread = keep.tile([P, FEATURES], BF16)
+        zero_codes = keep.tile([P, FEATURES // PACK], U32, align_bytes=64)
+        zero_scales = keep.tile([P, FEATURES // PACK], U8, align_bytes=64)
         centred = keep.tile([P, TOKEN_TILES, FEATURES], F32)
         neg_mean = keep.tile([P, TOKEN_TILES], F32)
         sq_sum = keep.tile([P, TOKEN_TILES], F32)
@@ -129,6 +131,7 @@ def tile_dcadecoderblock_pb_kernel(
             nc.sync.dma_start(out=x_raw[:, i, :], in_=x_rows[i * P : (i + 1) * P, :])
 
         nc.vector.memset(vec_rows[:].bitcast(I32), 0)
+        nc.vector.quantize_mx(out=zero_codes[:].bitcast(FP8X4), scales=zero_scales[:], in_=vec_rows[:])
         load_weight(0)
         load_vectors()
         load_weight(1)
@@ -193,6 +196,19 @@ def tile_dcadecoderblock_pb_kernel(
                     nc.tensor.transpose(
                         flipped[i][:, piece : piece + P], h_words[:, i, g, u, :], ident[:]
                     )
+
+        def warm_up(passes):
+            idle = bank_tile(sums_bank(0, 1), [P, FEATURES // PACK], F32)
+            for k in range(passes):
+                nc.tensor.matmul_mx(
+                    out=idle[:],
+                    lhsT=zero_codes[:, 0:P].bitcast(FP8X4),
+                    lhsT_scale=zero_scales[:, 0:P],
+                    rhs=zero_codes[:].bitcast(FP8X4),
+                    rhs_scale=zero_scales[:],
+                    start=(k == 0),
+                    stop=(k == passes - 1),
+                )
 
         def collect(copy, i):
             copy(
@@ -418,6 +434,7 @@ def tile_dcadecoderblock_pb_kernel(
                 out=out_rows[TURNED * P : (TURNED + 1) * P, half(c)], in_=result[:, TURNED, half(c)]
             )
 
+        warm_up(8)
         regroup_on_vector(0)
         regroup_on_scalar(0)
         vec_t = bank_tile(columns_bank, [P, BLOCKS, P], BF16)
@@ -431,6 +448,7 @@ def tile_dcadecoderblock_pb_kernel(
         regroup_on_scalar(1)
         quantise(0)
         quantise(1)
+        warm_up(4)
         flip(0)
         flip(1)
         flip(2)

@@ -497,12 +497,12 @@ def tile_dcadecoderblock_pb_kernel(
             add_bias(0, c)
         mean(0)
         deviation(0)
-        nc.sync.dma_start(out=gain_all[:], in_=attn_norm_g.partition_broadcast(P))
         normalise()
         gain_bank = spread(GAIN)
         for c in halves:
             add_bias(2, c)
         add_shift(2)
+        nc.vector.tensor_copy(out=gain_all[:], in_=gain_bank[:])
         for c in halves:
             add_bias_centred(1, c)
         gain_on_gpsimd(1, proj)

@@ -197,8 +197,8 @@ def tile_dcadecoderblock_pb_kernel(
                         flipped[i][:, piece : piece + P], h_words[:, i, g, u, :], ident[:]
                     )
 
-        def warm_up(passes):
-            idle = bank_tile(sums_bank(0, 1), [P, FEATURES // PACK], F32)
+        def warm_up(passes, bank=sums_bank(0, 1)):
+            idle = bank_tile(bank, [P, FEATURES // PACK], F32)
             for k in range(passes):
                 nc.tensor.matmul_mx(
                     out=idle[:],
@@ -502,9 +502,9 @@ def tile_dcadecoderblock_pb_kernel(
         for c in halves:
             add_bias(2, c)
         add_shift(2)
-        nc.vector.tensor_copy(out=gain_all[:], in_=gain_bank[:])
         for c in halves:
             add_bias_centred(1, c)
+        nc.vector.tensor_copy(out=gain_all[:], in_=gain_bank[:])
         gain_on_gpsimd(1, proj)
         mean(2)
         mean_of_sums(3)
@@ -513,10 +513,12 @@ def tile_dcadecoderblock_pb_kernel(
             add_bias_centred(3, c)
         gain_on_gpsimd(3, proj)
         deviation(2)
+        warm_up(6)
         there = [turn_there(c) for c in halves]
         add_shift(1)
         deviation_centred(1)
         gain_and_shift(0, there[0])
+        warm_up(4, sums_bank(3, 1))
         back = {}
         back[0] = turn_back(0)
         gain_and_shift(1, there[1])

@@ -88,7 +88,8 @@ def tile_dcadecoderblock_pb_kernel(
         affine_t = keep.tile([P, BLOCKS, P], F32)
         result = keep.tile([P, TOKEN_TILES, FEATURES], F32)
         squares = keep.tile([P, TOKEN_TILES, FEATURES], BF16)
-        vec_rows = keep.tile([P, FEATURES], BF16, align_bytes=64)
+        zeros = keep.tile([P, FEATURES], BF16, align_bytes=64)
+        vec_rows = keep.tile([P, FEATURES], BF16)
         bias_all = keep.tile([P, FEATURES], BF16)
         ident = keep.tile([P, P], F32)
         ident_bf = keep.tile([P, P], BF16)
@@ -131,7 +132,8 @@ def tile_dcadecoderblock_pb_kernel(
             nc.sync.dma_start(out=x_raw[:, i, :], in_=x_rows[i * P : (i + 1) * P, :])
 
         nc.vector.memset(vec_rows[:].bitcast(I32), 0)
-        nc.vector.quantize_mx(out=zero_codes[:].bitcast(FP8X4), scales=zero_scales[:], in_=vec_rows[:])
+        nc.vector.memset(zeros[:].bitcast(I32), 0)
+        nc.vector.quantize_mx(out=zero_codes[:].bitcast(FP8X4), scales=zero_scales[:], in_=zeros[:])
         load_weight(0)
         load_vectors()
         load_weight(1)
@@ -379,17 +381,16 @@ def tile_dcadecoderblock_pb_kernel(
                 op1=ALU.mult,
             )
 
-        def finish(i):
-            for c in halves:
-                nc.vector.scalar_tensor_tensor(
-                    out=result[:, i, half(c)],
-                    in0=scaled[:, i, half(c)],
-                    scalar=rstd[:, i : i + 1],
-                    in1=shifted[i, c][:],
-                    op0=ALU.mult,
-                    op1=ALU.add,
-                )
-                nc.sync.dma_start(out=out_rows[i * P : (i + 1) * P, half(c)], in_=result[:, i, half(c)])
+        def finish(i, c):
+            nc.vector.scalar_tensor_tensor(
+                out=result[:, i, half(c)],
+                in0=scaled[:, i, half(c)],
+                scalar=rstd[:, i : i + 1],
+                in1=shifted[i, c][:],
+                op0=ALU.mult,
+                op1=ALU.add,
+            )
+            nc.sync.dma_start(out=out_rows[i * P : (i + 1) * P, half(c)], in_=result[:, i, half(c)])
 
         def normalise():
             nc.gpsimd.tensor_scalar(
@@ -434,18 +435,16 @@ def tile_dcadecoderblock_pb_kernel(
                 out=out_rows[TURNED * P : (TURNED + 1) * P, half(c)], in_=result[:, TURNED, half(c)]
             )
 
-        warm_up(8)
+        warm_up(6)
         regroup_on_vector(0)
         regroup_on_scalar(0)
+        regroup_on_vector(1)
+        regroup_on_scalar(1)
         vec_t = bank_tile(columns_bank, [P, BLOCKS, P], BF16)
         for j in range(BLOCKS):
             nc.tensor.transpose(vec_t[:, j, :], vec_rows[:, j * P : (j + 1) * P], ident_bf[:])
         for cols in (vec_cols_bf, vec_cols):
             nc.scalar.copy(out=cols[:], in_=vec_t[:, :, 0 : SHIFT * QUADRANT + 1 : QUADRANT])
-        block_sums = bank_tile(columns_bank, [P, BLOCKS], F32)
-        nc.tensor.matmul(out=block_sums[:], lhsT=ones[:], rhs=vec_cols_bf[:, :, BIAS], start=True, stop=True)
-        regroup_on_vector(1)
-        regroup_on_scalar(1)
         quantise(0)
         quantise(1)
         warm_up(4)
@@ -453,6 +452,8 @@ def tile_dcadecoderblock_pb_kernel(
         flip(1)
         flip(2)
         flip(3)
+        block_sums = bank_tile(columns_bank, [P, BLOCKS], F32)
+        nc.tensor.matmul(out=block_sums[:], lhsT=ones[:], rhs=vec_cols_bf[:, :, BIAS], start=True, stop=True)
         collect(nc.scalar.copy, 0)
         collect(nc.scalar.copy, 1)
         collect(nc.scalar.copy, 2)
@@ -509,10 +510,12 @@ def tile_dcadecoderblock_pb_kernel(
         mean(2)
         mean_of_sums(3)
         centre_and_gain(2)
-        for c in halves:
-            add_bias_centred(3, c)
-        gain_on_gpsimd(3, proj)
         deviation(2)
+        add_bias_centred(3, 0)
+        finish(2, 0)
+        add_bias_centred(3, 1)
+        gain_on_gpsimd(3, proj)
+        finish(2, 1)
         warm_up(6)
         there = [turn_there(c) for c in halves]
         add_shift(1)
@@ -525,8 +528,9 @@ def tile_dcadecoderblock_pb_kernel(
         back[1] = turn_back(1)
         deviation_centred(3)
         add_shift(3)
-        finish(2)
-        finish(1)
+        for c in halves:
+            finish(1, c)
         for c in halves:
             add_x(c, back[c])
-        finish(3)
+        for c in halves:
+            finish(3, c)

from contextlib import ExitStack

import concourse.mybir as mybir
from concourse.masks import make_identity

F32 = mybir.dt.float32
BF16 = mybir.dt.bfloat16
I32 = mybir.dt.int32
U32 = mybir.dt.uint32
U8 = mybir.dt.uint8
FP8X4 = mybir.dt.float8_e4m3fn_x4
ALU = mybir.AluOpType
ACT = mybir.ActivationFunctionType

P = 128
PACK = 4
PAIR = 2
K_PASS = P * PACK
TOKENS = 512
K = 1024
FEATURES = 1024
EPS = 1e-5
TOKEN_TILES = TOKENS // P
PASSES = K // K_PASS
BANK = 512
PSUM_BANKS = 8
HALVES = FEATURES // BANK
UNITS = PASSES * HALVES
BLOCKS = FEATURES // P
BANK_BLOCKS = BANK // P
RUN = 8
QUADRANT = 32
BIAS, GAIN, SHIFT = 0, 1, 2
VECTORS = 3
VECTOR_SHARE = (320, 320, 320, 320)
TURNED = 0
FLOPS = 2 * TOKENS * K * FEATURES


def tile_dcadecoderblock_pb_kernel(
    tc, h_attn, x, attn_out_W, attn_out_b, attn_norm_g, attn_norm_b, out
):
    nc = tc.nc
    h_rows = h_attn.flatten_outer_dims()
    x_rows = x.flatten_outer_dims()
    out_rows = out.flatten_outer_dims()
    tiles = range(TOKEN_TILES)
    halves = range(HALVES)
    first_pass = range(HALVES)
    last_pass = range(UNITS - HALVES, UNITS)

    with ExitStack() as ctx:
        keep = ctx.enter_context(tc.tile_pool(name="keep", bufs=1))
        psum = ctx.enter_context(tc.psum_pool(name="psum", bufs=1))

        def bank_tile(k, shape, dtype):
            return psum.tile(shape, dtype, tag="bank%d" % k, name="bank%d" % k)

        def sums_bank(i, c):
            return (HALVES * i + c + PSUM_BANKS - HALVES) % PSUM_BANKS

        columns_bank = sums_bank(3, 0)
        spread_bank = {BIAS: sums_bank(3, 1), GAIN: sums_bank(0, 0)}
        h_bank = 0
        turned_bank = (sums_bank(0, 1), sums_bank(1, 0))
        shifted_bank = {
            1: (sums_bank(1, 1), spread_bank[GAIN]),
            2: (sums_bank(2, 0), sums_bank(2, 1)),
            3: (sums_bank(3, 0), sums_bank(3, 1)),
        }

        ctx.enter_context(tc.manual_schedule())

        h_raw = keep.tile([P, TOKEN_TILES * K], BF16)
        h_grp = keep.tile([P, TOKEN_TILES * K], BF16, align_bytes=64)
        h_codes = keep.tile([P, TOKEN_TILES * PASSES * P], U32, align_bytes=64)
        h_scales = keep.tile([P, TOKEN_TILES * PASSES * P], U8, align_bytes=64)
        w_raw = keep.tile([P, UNITS, PACK, BANK], BF16)
        w_grp = keep.tile([P, UNITS, BANK, PACK], BF16, align_bytes=64)
        w_codes = keep.tile([P, UNITS, BANK], U32, align_bytes=64)
        w_scales = keep.tile([P, UNITS, BANK], U8, align_bytes=64)
        x_raw = keep.tile([P, TOKEN_TILES, FEATURES], BF16)
        proj = keep.tile([P, TOKEN_TILES, FEATURES], F32)
        scaled = keep.tile([P, TOKEN_TILES, FEATURES], F32)
        vec_cols = keep.tile([P, BLOCKS, VECTORS], F32)
        vec_cols_bf = keep.tile([P, BLOCKS, VECTORS], BF16)
        normed = keep.tile([P, FEATURES], F32)
        affine_t = keep.tile([P, BLOCKS, P], F32)
        result = keep.tile([P, TOKEN_TILES, FEATURES], F32)
        squares = keep.tile([P, TOKEN_TILES, FEATURES], BF16)
        zeros = keep.tile([P, FEATURES], BF16, align_bytes=64)
        vec_rows = keep.tile([P, FEATURES], BF16)
        bias_all = keep.tile([P, FEATURES], BF16)
        ident = keep.tile([P, P], F32)
        ident_bf = keep.tile([P, P], BF16)
        eps = keep.tile([P, 1], F32)
        warm = keep.tile([P, 1], F32)
        half_sum = keep.tile([P, TOKEN_TILES * HALVES], F32)
        half_mean = keep.tile([P, TOKEN_TILES * HALVES], F32)
        bias_sums = keep.tile([P, BLOCKS], F32)
        neg_bias = keep.tile([P, 1], F32)
        ones = keep.tile([P, P], BF16)
        gain_all = keep.tile([P, FEATURES], BF16)
        unread = keep.tile([P, FEATURES], BF16)
        zero_codes = keep.tile([P, FEATURES // PACK], U32, align_bytes=64)
        zero_scales = keep.tile([P, FEATURES // PACK], U8, align_bytes=64)
        centred = keep.tile([P, TOKEN_TILES, FEATURES], F32)
        neg_mean = keep.tile([P, TOKEN_TILES], F32)
        sq_sum = keep.tile([P, TOKEN_TILES], F32)
        rstd = keep.tile([P, TOKEN_TILES], F32)

        def load_weight(unit):
            g, c = divmod(unit, HALVES)
            nc.sync.dma_start(
                out=w_raw[:, unit, :, :],
                in_=attn_out_W[
                    g * K_PASS : (g + 1) * K_PASS, c * BANK : (c + 1) * BANK
                ].rearrange("(p t) c -> p t c", t=PACK),
            )

        def load_vectors():
            for v, vec in ((BIAS, attn_out_b), (GAIN, attn_norm_g), (SHIFT, attn_norm_b)):
                row = v * QUADRANT
                nc.sync.dma_start(
                    out=vec_rows[row : row + 1, :], in_=vec.rearrange("(o c) -> o c", o=1)
                )

        def load_tokens(i):
            nc.sync.dma_start(out=h_raw[:, i * K : (i + 1) * K], in_=h_rows[i * P : (i + 1) * P, :])

        def load_residual(i):
            nc.sync.dma_start(out=x_raw[:, i, :], in_=x_rows[i * P : (i + 1) * P, :])

        nc.vector.memset(vec_rows[:].bitcast(I32), 0)
        nc.vector.memset(zeros[:].bitcast(I32), 0)
        nc.vector.quantize_mx(out=zero_codes[:].bitcast(FP8X4), scales=zero_scales[:], in_=zeros[:])
        load_weight(0)
        load_vectors()
        load_weight(1)
        load_tokens(0)
        load_tokens(1)
        load_tokens(2)
        load_tokens(3)
        load_weight(2)
        load_weight(3)
        load_residual(0)
        load_residual(1)
        load_residual(2)
        load_residual(3)
        nc.vector.memset(eps[:], EPS)
        nc.vector.memset(ones[:], 1.0)
        make_identity(nc, ident[:])
        make_identity(nc, ident_bf[:])
        nc.scalar.activation(out=warm[:], in_=eps[:], func=ACT.Abs_reciprocal_sqrt)

        def regroup(copy, unit, lo, hi):
            copy(
                out=w_grp[:, unit, lo:hi, :].rearrange("p (c i) t -> p c t i", i=RUN),
                in_=w_raw[:, unit, :, lo:hi].rearrange("p t (c i) -> p c t i", i=RUN),
            )

        def regroup_on_vector(unit):
            regroup(nc.vector.tensor_copy, unit, 0, VECTOR_SHARE[unit])

        def regroup_on_scalar(unit):
            regroup(nc.scalar.copy, unit, VECTOR_SHARE[unit], BANK)

        def quantise(unit):
            nc.vector.quantize_mx(
                out=w_codes[:, unit, :].bitcast(FP8X4),
                scales=w_scales[:, unit, :],
                in_=w_grp[:, unit, :, :].rearrange("p c t -> p (c t)"),
            )

        def spread(v):
            everywhere = bank_tile(spread_bank[v], [P, FEATURES], BF16)
            for j in range(BLOCKS):
                nc.tensor.transpose(
                    everywhere[:, j * P : (j + 1) * P],
                    vec_cols_bf[:, j, v : v + 1].to_broadcast([P, P]),
                    ident_bf[:],
                )
            return everywhere

        h_words = h_raw[:].bitcast(F32).rearrange(
            "r (i g p u) -> r i g u p", i=TOKEN_TILES, g=PASSES, u=PAIR
        )
        h_grp_words = h_grp[:].bitcast(F32).rearrange(
            "p (i g r u) -> p i g r u", i=TOKEN_TILES, g=PASSES, u=PAIR
        )
        flipped = {}

        def flip(i):
            flipped[i] = bank_tile(h_bank + i, [P, BANK], F32)
            for g in range(PASSES):
                for u in range(PAIR):
                    piece = (g * PAIR + u) * P
                    nc.tensor.transpose(
                        flipped[i][:, piece : piece + P], h_words[:, i, g, u, :], ident[:]
                    )

        def warm_up(passes, bank=sums_bank(0, 1)):
            idle = bank_tile(bank, [P, FEATURES // PACK], F32)
            for k in range(passes):
                nc.tensor.matmul_mx(
                    out=idle[:],
                    lhsT=zero_codes[:, 0:P].bitcast(FP8X4),
                    lhsT_scale=zero_scales[:, 0:P],
                    rhs=zero_codes[:].bitcast(FP8X4),
                    rhs_scale=zero_scales[:],
                    start=(k == 0),
                    stop=(k == passes - 1),
                )

        def collect(copy, i):
            copy(
                out=h_grp_words[:, i],
                in_=flipped[i][:].rearrange("p (g u r) -> p g r u", g=PASSES, u=PAIR),
            )

        def quantise_tokens(i):
            words = slice(i * PASSES * P, (i + 1) * PASSES * P)
            nc.vector.quantize_mx(
                out=h_codes[:, words].bitcast(FP8X4),
                scales=h_scales[:, words],
                in_=h_grp[:, i * K : (i + 1) * K],
            )

        acc = {}

        def multiply(i, unit):
            g, c = divmod(unit, HALVES)
            if g == 0:
                acc[i, c] = bank_tile(sums_bank(i, c), [P, BANK], F32)
            words = slice((i * PASSES + g) * P, (i * PASSES + g + 1) * P)
            nc.tensor.matmul_mx(
                out=acc[i, c][:],
                lhsT=h_codes[:, words].bitcast(FP8X4),
                lhsT_scale=h_scales[:, words],
                rhs=w_codes[:, unit, :].bitcast(FP8X4),
                rhs_scale=w_scales[:, unit, :],
                start=(g == 0),
                stop=(g == PASSES - 1),
            )

        def half(c):
            return slice(c * BANK, (c + 1) * BANK)

        shifted = {}

        def add_shift(i):
            for c in halves:
                shifted[i, c] = bank_tile(shifted_bank[i][c], [P, BANK], F32)
                nc.tensor.matmul(
                    out=shifted[i, c][:], lhsT=ident_bf[:], rhs=x_raw[:, i, half(c)], start=True, stop=False
                )
                for b in range(BANK_BLOCKS):
                    j = c * BANK_BLOCKS + b
                    nc.tensor.matmul(
                        out=shifted[i, c][:, b * P : (b + 1) * P],
                        lhsT=vec_cols[:, j, SHIFT : SHIFT + 1].to_broadcast([P, P]),
                        rhs=ident[:],
                        is_transpose=True,
                        start=False,
                        stop=(b == BANK_BLOCKS - 1),
                    )

        def add_bias(i, c):
            nc.vector.scalar_tensor_tensor(
                out=proj[:, i, half(c)],
                in0=acc[i, c][:],
                scalar=1.0,
                in1=bias_all[:, half(c)],
                op0=ALU.mult,
                op1=ALU.add,
                accum_out=half_sum[:, i * HALVES + c : i * HALVES + c + 1],
            )

        def mean(i):
            both = slice(i * HALVES, (i + 1) * HALVES)
            nc.scalar.activation(
                out=half_mean[:, both],
                in_=half_sum[:, both],
                func=ACT.Copy,
                scale=-1.0 / FEATURES,
                accum_out=neg_mean[:, i : i + 1],
            )

        def mean_of_sums(i):
            for c in halves:
                nc.scalar.activation(
                    out=unread[:, half(c)],
                    in_=acc[i, c][:],
                    func=ACT.Copy,
                    scale=-1.0 / FEATURES,
                    accum_out=half_sum[:, i * HALVES + c : i * HALVES + c + 1],
                )
            both = slice(i * HALVES, (i + 1) * HALVES)
            nc.scalar.activation(
                out=half_mean[:, both],
                in_=half_sum[:, both],
                func=ACT.Identity,
                bias=neg_bias[:],
                scale=1.0,
                accum_out=neg_mean[:, i : i + 1],
            )

        def add_bias_centred(i, c):
            nc.vector.scalar_tensor_tensor(
                out=proj[:, i, half(c)],
                in0=acc[i, c][:],
                scalar=neg_mean[:, i : i + 1],
                in1=bias_all[:, half(c)],
                op0=ALU.add,
                op1=ALU.add,
            )

        def deviation_centred(i):
            nc.scalar.activation(
                out=squares[:, i, :],
                in_=proj[:, i, :],
                func=ACT.Square,
                accum_out=sq_sum[:, i : i + 1],
            )
            nc.scalar.activation(
                out=rstd[:, i : i + 1],
                in_=sq_sum[:, i : i + 1],
                func=ACT.Abs_reciprocal_sqrt,
                bias=eps[:],
                scale=1.0 / FEATURES,
            )

        def centre_on_scalar(i):
            nc.scalar.activation(
                out=centred[:, i, :],
                in_=proj[:, i, :],
                func=ACT.Identity,
                bias=neg_mean[:, i : i + 1],
                scale=1.0,
            )

        def centre_on_gpsimd(i, lo=0, hi=FEATURES):
            nc.gpsimd.tensor_scalar(
                out=centred[:, i, lo:hi],
                in0=proj[:, i, lo:hi],
                scalar1=neg_mean[:, i : i + 1],
                scalar2=1.0,
                op0=ALU.add,
                op1=ALU.mult,
            )

        def gain_on_gpsimd(i, source, lo=0, hi=FEATURES):
            nc.gpsimd.tensor_tensor(
                out=scaled[:, i, lo:hi], in0=source[:, i, lo:hi], in1=gain_all[:, lo:hi], op=ALU.mult
            )

        def deviation(i):
            nc.scalar.activation(
                out=squares[:, i, :],
                in_=proj[:, i, :],
                func=ACT.Square,
                bias=neg_mean[:, i : i + 1],
                scale=1.0,
                accum_out=sq_sum[:, i : i + 1],
            )
            nc.scalar.activation(
                out=rstd[:, i : i + 1],
                in_=sq_sum[:, i : i + 1],
                func=ACT.Abs_reciprocal_sqrt,
                bias=eps[:],
                scale=1.0 / FEATURES,
            )

        def centre_and_gain(i, lo=0, hi=FEATURES):
            nc.vector.scalar_tensor_tensor(
                out=scaled[:, i, lo:hi],
                in0=proj[:, i, lo:hi],
                scalar=neg_mean[:, i : i + 1],
                in1=gain_bank[:, lo:hi],
                op0=ALU.add,
                op1=ALU.mult,
            )

        def finish(i, c):
            nc.vector.scalar_tensor_tensor(
                out=result[:, i, half(c)],
                in0=scaled[:, i, half(c)],
                scalar=rstd[:, i : i + 1],
                in1=shifted[i, c][:],
                op0=ALU.mult,
                op1=ALU.add,
            )
            nc.sync.dma_start(out=out_rows[i * P : (i + 1) * P, half(c)], in_=result[:, i, half(c)])

        def normalise():
            nc.gpsimd.tensor_scalar(
                out=normed[:],
                in0=proj[:, TURNED, :],
                scalar1=neg_mean[:, TURNED : TURNED + 1],
                scalar2=rstd[:, TURNED : TURNED + 1],
                op0=ALU.add,
                op1=ALU.mult,
            )

        def turn_there(c):
            there = bank_tile(turned_bank[c], [P, BANK_BLOCKS, P], F32)
            for b in range(BANK_BLOCKS):
                j = c * BANK_BLOCKS + b
                nc.tensor.transpose(there[:, b, :], normed[:, j * P : (j + 1) * P], ident[:])
            return there

        def gain_and_shift(c, there):
            for b in range(BANK_BLOCKS):
                j = c * BANK_BLOCKS + b
                nc.scalar.activation(
                    out=affine_t[:, j, :],
                    in_=there[:, b, :],
                    func=ACT.Identity,
                    bias=vec_cols[:, j, SHIFT : SHIFT + 1],
                    scale=vec_cols[:, j, GAIN : GAIN + 1],
                )

        def turn_back(c):
            back = bank_tile(turned_bank[c], [P, BANK], F32)
            for b in range(BANK_BLOCKS):
                j = c * BANK_BLOCKS + b
                nc.tensor.transpose(back[:, b * P : (b + 1) * P], affine_t[:, j, :], ident[:])
            return back

        def add_x(c, back):
            nc.vector.tensor_tensor(
                out=result[:, TURNED, half(c)], in0=back[:], in1=x_raw[:, TURNED, half(c)], op=ALU.add
            )
            nc.sync.dma_start(
                out=out_rows[TURNED * P : (TURNED + 1) * P, half(c)], in_=result[:, TURNED, half(c)]
            )

        warm_up(6)
        regroup_on_vector(0)
        regroup_on_scalar(0)
        regroup_on_vector(1)
        regroup_on_scalar(1)
        vec_t = bank_tile(columns_bank, [P, BLOCKS, P], BF16)
        for j in range(BLOCKS):
            nc.tensor.transpose(vec_t[:, j, :], vec_rows[:, j * P : (j + 1) * P], ident_bf[:])
        for cols in (vec_cols_bf, vec_cols):
            nc.scalar.copy(out=cols[:], in_=vec_t[:, :, 0 : SHIFT * QUADRANT + 1 : QUADRANT])
        quantise(0)
        quantise(1)
        warm_up(4)
        flip(0)
        flip(1)
        flip(2)
        flip(3)
        block_sums = bank_tile(columns_bank, [P, BLOCKS], F32)
        nc.tensor.matmul(out=block_sums[:], lhsT=ones[:], rhs=vec_cols_bf[:, :, BIAS], start=True, stop=True)
        collect(nc.scalar.copy, 0)
        collect(nc.scalar.copy, 1)
        collect(nc.scalar.copy, 2)
        collect(nc.scalar.copy, 3)
        nc.scalar.activation(
            out=bias_sums[:],
            in_=block_sums[:],
            func=ACT.Copy,
            scale=-1.0 / (HALVES * FEATURES),
            accum_out=neg_bias[:],
        )
        quantise_tokens(0)
        multiply(0, 0)
        multiply(0, 1)
        quantise_tokens(1)
        multiply(1, 0)
        multiply(1, 1)
        bias_bank = spread(BIAS)
        regroup_on_vector(2)
        regroup_on_scalar(2)
        quantise_tokens(2)
        multiply(2, 0)
        multiply(2, 1)
        quantise_tokens(3)
        regroup_on_scalar(3)
        regroup_on_vector(3)
        nc.scalar.copy(out=bias_all[:], in_=bias_bank[:])
        quantise(2)
        multiply(0, 2)
        multiply(1, 2)
        multiply(2, 2)
        quantise(3)
        multiply(0, 3)
        multiply(1, 3)
        multiply(2, 3)
        multiply(3, 0)
        multiply(3, 1)
        multiply(3, 2)
        multiply(3, 3)
        mean_of_sums(1)
        for c in halves:
            add_bias(0, c)
        mean(0)
        deviation(0)
        normalise()
        gain_bank = spread(GAIN)
        for c in halves:
            add_bias(2, c)
        add_shift(2)
        for c in halves:
            add_bias_centred(1, c)
        nc.vector.tensor_copy(out=gain_all[:], in_=gain_bank[:])
        gain_on_gpsimd(1, proj)
        mean(2)
        mean_of_sums(3)
        centre_and_gain(2)
        deviation(2)
        add_bias_centred(3, 0)
        finish(2, 0)
        add_bias_centred(3, 1)
        gain_on_gpsimd(3, proj)
        finish(2, 1)
        warm_up(6)
        there = [turn_there(c) for c in halves]
        add_shift(1)
        deviation_centred(1)
        gain_and_shift(0, there[0])
        warm_up(4, sums_bank(3, 1))
        back = {}
        back[0] = turn_back(0)
        gain_and_shift(1, there[1])
        back[1] = turn_back(1)
        deviation_centred(3)
        add_shift(3)
        for c in halves:
            finish(1, c)
        for c in halves:
            add_x(c, back[c])
        for c in halves:
            finish(3, c)
